import numpy as np
import ml_dtypes


def mxq(x, axis, fmt="e4m3"):
    dtype, down = {"e4m3": (ml_dtypes.float8_e4m3fn, 7), "e5m2": (ml_dtypes.float8_e5m2, 14)}[fmt]
    v = np.moveaxis(np.asarray(x, np.float32).astype(ml_dtypes.bfloat16).astype(np.float64), axis, -1)
    blocks = v.reshape(v.shape[:-1] + (-1, 32))
    amax = np.abs(blocks).max(-1, keepdims=True)
    byte = np.maximum(np.where(amax > 0, np.frexp(amax)[1] - 1 + 127, 0) - down, 1)
    scale = np.exp2(byte - 127.0)
    codes = (blocks / scale).astype(np.float32).astype(dtype).astype(np.float64)
    return np.moveaxis((codes * scale).reshape(v.shape), -1, axis)


WIDE = False


def mx_kscale(k):
    if not WIDE:
        return np.ones(k)
    levels = np.array([30, -30])
    if k % 512:
        return np.exp2(np.random.permutation(np.resize(levels, k // 32))).repeat(32)
    a = np.empty((k // 512, 16))
    for p in range(k // 512):
        a[p, :8] = np.random.permutation(np.resize(levels, 8))
        for g in range(8):
            far = levels[np.abs(levels - a[p, g]) >= 10]
            a[p, g + 8] = far[np.random.randint(len(far))]
    return np.exp2(a.ravel()).repeat(32)


BF16 = ml_dtypes.bfloat16


def bf(x):
    return np.asarray(x, np.float32).astype(BF16)


def f64(x):
    return np.asarray(x).astype(np.float64)


T, M, HW, D, DK, H = 2, 512, 768, 1024, 1024, 8
EPS = 1e-6
EXTENT = 27.0


def rope_2d(x, pos):
    nt, n, c = x.shape
    half, quarter = c // 2, c // 4
    theta = 100.0 ** (-2.0 * np.arange(quarter) / half)

    def apply(part, p):
        fr = p[..., None] * theta
        cos, sin = np.cos(fr), np.sin(fr)
        pr = part.reshape(nt, n, quarter, 2)
        x1, x2 = pr[..., 0], pr[..., 1]
        return np.stack([x1 * cos - x2 * sin, x1 * sin + x2 * cos], axis=-1).reshape(nt, n, half)

    return np.concatenate([apply(x[:, :, :half], pos[..., 0]), apply(x[:, :, half:], pos[..., 1])], axis=-1)


def layernorm_nobias(x, gamma):
    mu = x.mean(-1, keepdims=True)
    var = ((x - mu) ** 2).mean(-1, keepdims=True)
    return (x - mu) / np.sqrt(var + EPS) * gamma


def setup_inputs():
    s = mx_kscale(D)
    return {"updated_track_tokens": bf(np.random.standard_normal((T, M, D)) * s),
            "tracks": bf(np.random.uniform(0.0, EXTENT, (T, M, 2))),
            "W_k": bf(np.random.standard_normal((DK, D)) / np.sqrt(D) / s),
            "k_gamma": bf(1.0 + 0.1 * np.random.standard_normal(DK))}


def reference(updated_track_tokens, tracks, W_k, k_gamma):
    k = mxq(f64(updated_track_tokens), 2, "e5m2") @ mxq(f64(W_k), 1, "e5m2").T
    k = rope_2d(k, f64(tracks))
    return layernorm_nobias(k, f64(k_gamma))

@@ -1,0 +1,285 @@
+import math
+from contextlib import ExitStack
+
+import concourse.mybir as mybir
+from concourse.masks import make_identity
+
+T, M, D, DK = 2, 512, 1024, 1024
+EPS = 1e-6
+FLOPS = 2 * T * M * D * DK
+
+F32 = mybir.dt.float32
+BF16 = mybir.dt.bfloat16
+I32 = mybir.dt.int32
+U32 = mybir.dt.uint32
+U8 = mybir.dt.uint8
+E5M2X4 = mybir.dt.float8_e5m2_x4
+ALU = mybir.AluOpType
+ACT = mybir.ActivationFunctionType
+
+P = 128
+TILES = T * M // P
+PASSES = D // 512
+PAIRS = DK // 2
+FREQS = PAIRS // 2
+W_LOADS = PAIRS // P
+LAST = TILES - 1
+G_GAIN = 0
+G_NORM = 512
+LAG = 3
+
+
+def tile_attentionalsplatting_pa_kernel(tc, updated_track_tokens, tracks, W_k, k_gamma, out):
+    nc = tc.nc
+    x_rows = updated_track_tokens.flatten_outer_dims().rearrange("(p j) k -> p j k", j=TILES)
+    pos_rows = tracks.flatten_outer_dims().rearrange("(p j) c -> p (j c)", j=TILES)
+    out_rows = out.flatten_outer_dims().rearrange("(p j) n -> p j n", j=TILES)
+    w_rows = W_k.rearrange("(q p e) k -> q p e k", p=P, e=2)
+
+    with ExitStack() as ctx:
+        keep = ctx.enter_context(tc.tile_pool(name="keep", bufs=1))
+        work = ctx.enter_context(tc.tile_pool(name="work", bufs=3))
+        psum = ctx.enter_context(tc.psum_pool(name="psum", bufs=1))
+        ctx.enter_context(tc.manual_schedule())
+
+        gamma_rows = keep.tile([P, DK], BF16, name="gamma_rows")
+        nc.vector.memset(gamma_rows[:], 0.0)
+        pos_bf = keep.tile([P, 2 * TILES], BF16, name="pos_bf")
+        nc.scalar.dma_start(out=pos_bf[:], in_=pos_rows)
+        nc.scalar.dma_start(out=gamma_rows[0:1, :], in_=k_gamma.rearrange("(o n) -> o n", o=1))
+
+        w_raw = [keep.tile([P, 2, D], BF16, name="w_raw%d" % q) for q in range(W_LOADS)]
+        x_groups = [(0, 1), (1, 2), (2, 4), (4, 6), (6, 8)]
+        x_raw = [keep.tile([P, b - a, D], BF16, name="x_raw%d" % a) for a, b in x_groups]
+        x_src = {}
+        for (a, b), t in zip(x_groups, x_raw):
+            for j in range(a, b):
+                x_src[j] = t[:, j - a, :]
+        for q in range(W_LOADS - 1):
+            nc.sync.dma_start(out=w_raw[q][:], in_=w_rows[q])
+        nc.sync.dma_start(out=x_raw[0][:], in_=x_rows[:, 0:1, :])
+        nc.sync.dma_start(out=w_raw[W_LOADS - 1][:], in_=w_rows[W_LOADS - 1])
+        for (a, b), t in list(zip(x_groups, x_raw))[1:]:
+            nc.sync.dma_start(out=t[:], in_=x_rows[:, a:b, :])
+
+        ident = keep.tile([P, P], F32, name="ident")
+        make_identity(nc, ident[:])
+        ones = keep.tile([P, P], BF16, name="ones")
+        nc.gpsimd.memset(ones[:], 1.0)
+        minus_half = keep.tile([P, 1], F32, name="minus_half")
+        nc.gpsimd.memset(minus_half[:], -0.5)
+
+        one = keep.tile([P, 1], F32, name="one")
+        nc.vector.memset(one[:], 1.0)
+        turns = keep.tile([P, FREQS], F32, name="turns")
+        for i in range(4):
+            nc.vector.tensor_scalar(out=turns[:, i : i + 1], in0=one[:], scalar1=100.0 ** (-i / FREQS) / (2 * math.pi), scalar2=None, op0=ALU.mult)
+        for width in (4, 16, 64):
+            for m in (1, 2, 3):
+                nc.vector.tensor_scalar(out=turns[:, m * width : (m + 1) * width], in0=turns[:, 0:width], scalar1=100.0 ** (-m * width / FREQS), scalar2=None, op0=ALU.mult)
+        pos = keep.tile([P, 2 * TILES], F32, name="pos")
+        nc.vector.tensor_copy(out=pos[:], in_=pos_bf[:])
+
+
+        w_codes = keep.tile([P, 2, PASSES, PAIRS], U32, name="w_codes", align_bytes=64)
+        w_scales = keep.tile([P, 2, PASSES, PAIRS], U8, name="w_scales", align_bytes=64)
+        x_codes = [keep.tile([P, PASSES * P], U32, name="x_codes%d" % j, align_bytes=64) for j in range(TILES)]
+        x_scales = [keep.tile([P, PASSES * P], U8, name="x_scales%d" % j, align_bytes=64) for j in range(TILES)]
+        frac = [keep.tile([P, PAIRS], F32, name="frac%d" % j) for j in range(TILES)]
+        sums = [keep.tile([P, 4], F32, name="sums%d" % j) for j in range(TILES)]
+        neg_mean = [keep.tile([P, 1], F32, name="neg_mean%d" % j) for j in range(TILES)]
+        sum_sq = [keep.tile([P, 1], F32, name="sum_sq%d" % j) for j in range(TILES)]
+        rstd = [keep.tile([P, 1], F32, name="rstd%d" % j) for j in range(TILES)]
+        var, result = {}, {}
+        banks, staged, sin, cos, fold, acc, rot, cross = {}, {}, {}, {}, {}, {}, {}, {}
+
+        def transpose(key, rows):
+            words = rows.bitcast(F32)
+            banks[key] = psum.tile([P, PASSES, 2, P], F32, name="turned", bufs=3)
+            for g in range(PASSES):
+                for u in range(2):
+                    nc.tensor.transpose(banks[key][:, g, u, :], words[:, 256 * g + u : 256 * (g + 1) : 2], ident[:])
+
+        def copy_out(key):
+            staged[key] = work.tile([P, D], BF16, name="staged", bufs=4, align_bytes=64)
+            nc.scalar.copy(out=staged[key][:].bitcast(F32).rearrange("p (g r u) -> p g r u", g=PASSES, u=2), in_=banks[key][:].rearrange("p g u r -> p g r u"))
+
+        def quantize_w(q, e):
+            for g in range(PASSES):
+                cols = slice(q * P, (q + 1) * P)
+                nc.vector.quantize_mx(out=w_codes[:, e, g, cols].bitcast(E5M2X4), scales=w_scales[:, e, g, cols], in_=staged[q, e][:, 512 * g : 512 * (g + 1)])
+
+        def quantize_x(j):
+            nc.vector.quantize_mx(out=x_codes[j][:].bitcast(E5M2X4), scales=x_scales[j][:], in_=staged[j][:])
+
+        def reduce_angles(j):
+            whole = work.tile([P, PAIRS], I32, name="whole", bufs=2)
+            for h in range(2):
+                nc.vector.tensor_scalar(out=whole[:, h * FREQS : (h + 1) * FREQS], in0=turns[:], scalar1=pos[:, 2 * j + h : 2 * j + h + 1], scalar2=None, op0=ALU.mult)
+            for h in range(2):
+                cols = slice(h * FREQS, (h + 1) * FREQS)
+                nc.vector.scalar_tensor_tensor(out=frac[j][:, cols], in0=turns[:], scalar=pos[:, 2 * j + h : 2 * j + h + 1], in1=whole[:, cols], op0=ALU.mult, op1=ALU.subtract)
+
+        def sine(j):
+            sin[j] = work.tile([P, PAIRS], F32, name="sin", bufs=3)
+            nc.scalar.activation(out=sin[j][:], in_=frac[j][:], func=ACT.Sin, scale=2 * math.pi)
+
+        def absolute(j):
+            fold[j] = work.tile([P, PAIRS], F32, name="fold", bufs=2)
+            nc.scalar.activation(out=fold[j][:], in_=frac[j][:], func=ACT.Abs)
+
+        def cosine(j):
+            cos[j] = work.tile([P, PAIRS], F32, name="cos", bufs=3)
+            nc.scalar.activation(out=cos[j][:], in_=fold[j][:], func=ACT.Sin, scale=-2 * math.pi, bias=math.pi / 2)
+
+        def project(j):
+            for e in range(2):
+                acc[j, e] = psum.tile([P, PAIRS], F32, name="acc%d" % e, bufs=2)
+                for g in range(PASSES):
+                    cols = slice(g * P, (g + 1) * P)
+                    nc.tensor.matmul_mx(out=acc[j, e][:], lhsT=x_codes[j][:, cols].bitcast(E5M2X4), lhsT_scale=x_scales[j][:, cols], rhs=w_codes[:, e, g, :].bitcast(E5M2X4), rhs_scale=w_scales[:, e, g, :], start=(g == 0), stop=(g == PASSES - 1))
+
+        def multiply(j):
+            rot[j] = work.tile([P, 2, PAIRS], F32, name="rot", bufs=4)
+            cross[j] = work.tile([P, 2, PAIRS], F32, name="cross")
+            terms = ((rot[j][:, 0, :], 0, 1.0, cos), (cross[j][:, 0, :], 1, -1.0, sin), (rot[j][:, 1, :], 1, 1.0, cos), (cross[j][:, 1, :], 0, 1.0, sin))
+            for n, (dst, e, sign, table) in enumerate(terms):
+                nc.vector.scalar_tensor_tensor(out=dst, in0=acc[j, e][:], scalar=sign, in1=table[j][:], op0=ALU.mult, op1=ALU.mult, accum_out=sums[j][:, n : n + 1])
+
+        def mean(j):
+            parts = work.tile([P, 4], F32, name="parts")
+            nc.scalar.activation(out=parts[:], in_=sums[j][:], func=ACT.Identity, scale=-1.0 / DK, accum_out=neg_mean[j][:])
+
+        def add(j):
+            nc.gpsimd.tensor_tensor(out=rot[j][:], in0=rot[j][:], in1=cross[j][:], op=ALU.add)
+
+        def add_centred(j):
+            nc.vector.scalar_tensor_tensor(out=rot[j][:], in0=rot[j][:], scalar=neg_mean[j][:], in1=cross[j][:], op0=ALU.add, op1=ALU.add)
+
+        def square(j):
+            bias = 0.0 if j == LAST else neg_mean[j][:]
+            nc.scalar.activation(out=cross[j][:], in_=rot[j][:], func=ACT.Square, bias=bias, accum_out=sum_sq[j][:])
+
+        def variance(j):
+            var[j] = work.tile([P, 1], F32, name="var")
+            nc.scalar.activation(out=var[j][:], in_=sum_sq[j][:], func=ACT.Identity, scale=1.0 / DK, bias=EPS)
+
+        def inverse_std(j):
+            nc.gpsimd.tensor_tensor(out=rstd[j][:], in0=var[j][:], in1=minus_half[:], op=ALU.pow)
+
+        def paired(j, lo, hi):
+            return rot[j][:, :, lo // 2 : hi // 2].rearrange("p e c -> p c e")
+
+        def normalise(j):
+            result[j] = work.tile([P, DK], F32, name="result", bufs=4)
+            shift = work.tile([P, 1], F32, name="shift")
+            nc.scalar.activation(out=shift[:], in_=neg_mean[j][:], func=ACT.Identity, scale=rstd[j][:])
+            if G_NORM:
+                nc.gpsimd.tensor_scalar(out=result[j][:, :G_NORM], in0=paired(j, 0, G_NORM), scalar1=neg_mean[j][:], scalar2=rstd[j][:], op0=ALU.add, op1=ALU.mult)
+            return shift
+
+        def normalise2(j, shift):
+            nc.scalar.activation(out=result[j][:, G_NORM:], in_=paired(j, G_NORM, DK), func=ACT.Identity, scale=rstd[j][:], bias=shift[:])
+
+        def gain_gpsimd(j, c):
+            if c:
+                nc.gpsimd.tensor_tensor(out=result[j][:, :c], in0=result[j][:, :c], in1=gamma_sb[:, :c], op=ALU.mult)
+
+        def finish(j, c):
+            if c < DK:
+                nc.vector.tensor_tensor(out=result[j][:, c:], in0=result[j][:, c:], in1=gamma[:, c:], op=ALU.mult)
+            nc.sync.dma_start(out=out_rows[:, j, :], in_=result[j][:])
+
+        def finish_last(j):
+            result[j] = work.tile([P, DK], F32, name="result", bufs=4)
+            for lo in (0, DK // 2):
+                cols = slice(lo, lo + DK // 2)
+                nc.vector.scalar_tensor_tensor(out=result[j][:, cols], in0=paired(j, lo, lo + DK // 2), scalar=rstd[j][:], in1=gamma[:, cols], op0=ALU.mult, op1=ALU.mult)
+                nc.sync.dma_start(out=out_rows[:, j, cols], in_=result[j][:, cols])
+
+        reduce_angles(0)
+        reduce_angles(1)
+        reduce_angles(2)
+        w_tiles = [(q, e) for q in range(W_LOADS) for e in range(2)]
+        trig_first = [sine, absolute, cosine]
+        for n, (q, e) in enumerate(w_tiles):
+            if n == len(w_tiles) - 2:
+                transpose(0, x_src[0])
+                copy_out(0)
+                quantize_x(0)
+            transpose((q, e), w_raw[q][:, e, :])
+            if n < 3:
+                trig_first[n](0)
+            copy_out((q, e))
+            quantize_w(q, e)
+            if n in (0, 1, 3):
+                reduce_angles({0: 3, 1: 4, 3: 5}[n])
+        transpose(1, x_src[1])
+        copy_out(1)
+        project(0)
+        reduce_angles(6)
+        quantize_x(1)
+        absolute(1)
+        sine(1)
+        cosine(1)
+        transpose(2, x_src[2])
+        copy_out(2)
+        transpose(3, x_src[3])
+        copy_out(3)
+        reduce_angles(7)
+        project(1)
+        gamma = psum.tile([P, DK], BF16, name="gamma")
+        for half in range(2):
+            cols = slice(half * 512, (half + 1) * 512)
+            nc.tensor.matmul(gamma[:, cols], lhsT=ones[:], rhs=gamma_rows[:, cols], start=True, stop=True)
+        gains = {j: G_GAIN for j in range(TILES)}
+
+
+        for s in range(TILES):
+            ahead = [j for j in (2 * s + 4, 2 * s + 5) if j < TILES]
+            for j in ahead:
+                transpose(j, x_src[j])
+            multiply(s)
+            for j in (2 * s + 2, 2 * s + 3):
+                if j < TILES:
+                    quantize_x(j)
+            if s + 2 < TILES:
+                project(s + 2)
+                absolute(s + 2)
+                sine(s + 2)
+                cosine(s + 2)
+            for j in ahead:
+                copy_out(j)
+            if s == 1 and 0:
+                gamma_sb = keep.tile([P, 0], BF16, name="gamma_sb")
+                nc.scalar.copy(out=gamma_sb[:], in_=gamma[:, :0])
+            if s >= 2:
+                inverse_std(s - 2)
+            if s >= 1:
+                square(s - 1)
+            shift = normalise(s - 2) if s >= 2 else None
+            if s >= 3:
+                gain_gpsimd(s - 3, gains[s - 3])
+            if s == LAST:
+                mean(s)
+            if s >= 1:
+                variance(s - 1)
+            if s >= 2:
+                normalise2(s - 2, shift)
+            if s < LAST:
+                mean(s)
+                add(s)
+            if s >= 3:
+                finish(s - 3, gains[s - 3])
+        add_centred(LAST)
+        inverse_std(LAST - 1)
+        shift = normalise(LAST - 1)
+        square(LAST)
+        gain_gpsimd(LAST - 2, gains[LAST - 2])
+        finish(LAST - 2, gains[LAST - 2])
+        variance(LAST)
+        normalise2(LAST - 1, shift)
+        inverse_std(LAST)
+        gain_gpsimd(LAST - 1, gains[LAST - 1])
+        finish(LAST - 1, gains[LAST - 1])
+        finish_last(LAST)

@@ -26,7 +26,7 @@ W_LOADS = PAIRS // P
 LAST = TILES - 1
 G_GAIN = 0
 G_NORM = 512
-LAG = 3
+LAG = 2
 
 
 def tile_attentionalsplatting_pa_kernel(tc, updated_track_tokens, tracks, W_k, k_gamma, out):
@@ -139,26 +139,23 @@ def tile_attentionalsplatting_pa_kernel(tc, updated_track_tokens, tracks, W_k, k
                     cols = slice(g * P, (g + 1) * P)
                     nc.tensor.matmul_mx(out=acc[j, e][:], lhsT=x_codes[j][:, cols].bitcast(E5M2X4), lhsT_scale=x_scales[j][:, cols], rhs=w_codes[:, e, g, :].bitcast(E5M2X4), rhs_scale=w_scales[:, e, g, :], start=(g == 0), stop=(g == PASSES - 1))
 
-        def multiply(j):
-            rot[j] = work.tile([P, 2, PAIRS], F32, name="rot", bufs=4)
-            cross[j] = work.tile([P, 2, PAIRS], F32, name="cross")
-            terms = ((rot[j][:, 0, :], 0, 1.0, cos), (cross[j][:, 0, :], 1, -1.0, sin), (rot[j][:, 1, :], 1, 1.0, cos), (cross[j][:, 1, :], 0, 1.0, sin))
-            for n, (dst, e, sign, table) in enumerate(terms):
-                nc.vector.scalar_tensor_tensor(out=dst, in0=acc[j, e][:], scalar=sign, in1=table[j][:], op0=ALU.mult, op1=ALU.mult, accum_out=sums[j][:, n : n + 1])
+        def multiply(j, e):
+            if e == 0:
+                rot[j] = work.tile([P, 2, PAIRS], F32, name="rot", bufs=4)
+                cross[j] = work.tile([P, 2, PAIRS], F32, name="cross")
+            terms = ((rot[j][:, e, :], e, 1.0, cos), (cross[j][:, e, :], 1 - e, 2.0 * e - 1.0, sin))
+            for n, (dst, bank, sign, table) in enumerate(terms):
+                nc.vector.scalar_tensor_tensor(out=dst, in0=acc[j, bank][:], scalar=sign, in1=table[j][:], op0=ALU.mult, op1=ALU.mult, accum_out=sums[j][:, 2 * e + n : 2 * e + n + 1])
 
         def mean(j):
             parts = work.tile([P, 4], F32, name="parts")
             nc.scalar.activation(out=parts[:], in_=sums[j][:], func=ACT.Identity, scale=-1.0 / DK, accum_out=neg_mean[j][:])
 
-        def add(j):
-            nc.gpsimd.tensor_tensor(out=rot[j][:], in0=rot[j][:], in1=cross[j][:], op=ALU.add)
-
-        def add_centred(j):
-            nc.vector.scalar_tensor_tensor(out=rot[j][:], in0=rot[j][:], scalar=neg_mean[j][:], in1=cross[j][:], op0=ALU.add, op1=ALU.add)
+        def add(j, engine=nc.gpsimd, e=slice(0, 2)):
+            engine.tensor_tensor(out=rot[j][:, e, :], in0=rot[j][:, e, :], in1=cross[j][:, e, :], op=ALU.add)
 
         def square(j):
-            bias = 0.0 if j == LAST else neg_mean[j][:]
-            nc.scalar.activation(out=cross[j][:], in_=rot[j][:], func=ACT.Square, bias=bias, accum_out=sum_sq[j][:])
+            nc.scalar.activation(out=cross[j][:], in_=rot[j][:], func=ACT.Square, bias=neg_mean[j][:], accum_out=sum_sq[j][:])
 
         def variance(j):
             var[j] = work.tile([P, 1], F32, name="var")
@@ -170,33 +167,26 @@ def tile_attentionalsplatting_pa_kernel(tc, updated_track_tokens, tracks, W_k, k
         def paired(j, lo, hi):
             return rot[j][:, :, lo // 2 : hi // 2].rearrange("p e c -> p c e")
 
-        def normalise(j):
-            result[j] = work.tile([P, DK], F32, name="result", bufs=4)
-            shift = work.tile([P, 1], F32, name="shift")
-            nc.scalar.activation(out=shift[:], in_=neg_mean[j][:], func=ACT.Identity, scale=rstd[j][:])
-            if G_NORM:
-                nc.gpsimd.tensor_scalar(out=result[j][:, :G_NORM], in0=paired(j, 0, G_NORM), scalar1=neg_mean[j][:], scalar2=rstd[j][:], op0=ALU.add, op1=ALU.mult)
-            return shift
+        def centre_and_gain(j, lo=0, hi=DK):
+            if lo == 0:
+                result[j] = work.tile([P, DK], F32, name="result", bufs=4)
+            nc.vector.scalar_tensor_tensor(out=result[j][:, lo:hi], in0=paired(j, lo, hi), scalar=neg_mean[j][:], in1=gamma[:, lo:hi], op0=ALU.add, op1=ALU.mult)
 
-        def normalise2(j, shift):
-            nc.scalar.activation(out=result[j][:, G_NORM:], in_=paired(j, G_NORM, DK), func=ACT.Identity, scale=rstd[j][:], bias=shift[:])
+        def scale_gpsimd(j, lo, hi):
+            if hi > lo:
+                nc.gpsimd.tensor_scalar(out=result[j][:, lo:hi], in0=result[j][:, lo:hi], scalar1=rstd[j][:], scalar2=0.0, op0=ALU.mult, op1=ALU.add)
 
-        def gain_gpsimd(j, c):
-            if c:
-                nc.gpsimd.tensor_tensor(out=result[j][:, :c], in0=result[j][:, :c], in1=gamma_sb[:, :c], op=ALU.mult)
+        def scale_scalar(j, lo, hi):
+            if hi > lo:
+                nc.scalar.activation(out=result[j][:, lo:hi], in_=result[j][:, lo:hi], func=ACT.Identity, scale=rstd[j][:])
 
-        def finish(j, c):
-            if c < DK:
-                nc.vector.tensor_tensor(out=result[j][:, c:], in0=result[j][:, c:], in1=gamma[:, c:], op=ALU.mult)
-            nc.sync.dma_start(out=out_rows[:, j, :], in_=result[j][:])
+        def store(j, lo=0, hi=DK):
+            nc.sync.dma_start(out=out_rows[:, j, lo:hi], in_=result[j][:, lo:hi])
 
-        def finish_last(j):
-            result[j] = work.tile([P, DK], F32, name="result", bufs=4)
-            for lo in (0, DK // 2):
-                cols = slice(lo, lo + DK // 2)
-                nc.vector.scalar_tensor_tensor(out=result[j][:, cols], in0=paired(j, lo, lo + DK // 2), scalar=rstd[j][:], in1=gamma[:, cols], op0=ALU.mult, op1=ALU.mult)
-                nc.sync.dma_start(out=out_rows[:, j, cols], in_=result[j][:, cols])
-
+        gamma = psum.tile([P, DK], BF16, name="gamma")
+        for half in range(2):
+            cols = slice(half * 512, (half + 1) * 512)
+            nc.tensor.matmul(gamma[:, cols], lhsT=ones[:], rhs=gamma_rows[:, cols], start=True, stop=True)
         reduce_angles(0)
         reduce_angles(1)
         reduce_angles(2)
@@ -228,10 +218,6 @@ def tile_attentionalsplatting_pa_kernel(tc, updated_track_tokens, tracks, W_k, k
         copy_out(3)
         reduce_angles(7)
         project(1)
-        gamma = psum.tile([P, DK], BF16, name="gamma")
-        for half in range(2):
-            cols = slice(half * 512, (half + 1) * 512)
-            nc.tensor.matmul(gamma[:, cols], lhsT=ones[:], rhs=gamma_rows[:, cols], start=True, stop=True)
         gains = {j: G_GAIN for j in range(TILES)}
 
 
@@ -239,7 +225,18 @@ def tile_attentionalsplatting_pa_kernel(tc, updated_track_tokens, tracks, W_k, k
             ahead = [j for j in (2 * s + 4, 2 * s + 5) if j < TILES]
             for j in ahead:
                 transpose(j, x_src[j])
-            multiply(s)
+            share = G_NORM if s + 2 < TILES else 0
+            if s >= 3:
+                scale_scalar(s - 3, share, DK)
+                scale_gpsimd(s - 3, 0, share)
+                store(s - 3)
+            multiply(s, 0)
+            if s >= 2:
+                inverse_std(s - 2)
+            if s == LAST:
+                add(s, nc.gpsimd, slice(0, 1))
+                centre_and_gain(s - 2)
+            multiply(s, 1)
             for j in (2 * s + 2, 2 * s + 3):
                 if j < TILES:
                     quantize_x(j)
@@ -250,36 +247,32 @@ def tile_attentionalsplatting_pa_kernel(tc, updated_track_tokens, tracks, W_k, k
                 cosine(s + 2)
             for j in ahead:
                 copy_out(j)
-            if s == 1 and 0:
-                gamma_sb = keep.tile([P, 0], BF16, name="gamma_sb")
-                nc.scalar.copy(out=gamma_sb[:], in_=gamma[:, :0])
-            if s >= 2:
-                inverse_std(s - 2)
             if s >= 1:
                 square(s - 1)
-            shift = normalise(s - 2) if s >= 2 else None
-            if s >= 3:
-                gain_gpsimd(s - 3, gains[s - 3])
-            if s == LAST:
+            if s < LAST:
                 mean(s)
             if s >= 1:
                 variance(s - 1)
-            if s >= 2:
-                normalise2(s - 2, shift)
+            if 2 <= s < LAST:
+                centre_and_gain(s - 2)
             if s < LAST:
-                mean(s)
                 add(s)
-            if s >= 3:
-                finish(s - 3, gains[s - 3])
-        add_centred(LAST)
         inverse_std(LAST - 1)
-        shift = normalise(LAST - 1)
+        scale_scalar(LAST - 2, 0, DK)
+        store(LAST - 2)
+        mean(LAST)
+        add(LAST, nc.vector, slice(1, 2))
         square(LAST)
-        gain_gpsimd(LAST - 2, gains[LAST - 2])
-        finish(LAST - 2, gains[LAST - 2])
+        centre_and_gain(LAST - 1)
+        scale_gpsimd(LAST - 1, 0, 512)
         variance(LAST)
-        normalise2(LAST - 1, shift)
+        scale_scalar(LAST - 1, 512, DK)
+        store(LAST - 1)
         inverse_std(LAST)
-        gain_gpsimd(LAST - 1, gains[LAST - 1])
-        finish(LAST - 1, gains[LAST - 1])
-        finish_last(LAST)
+        half = DK // 2
+        centre_and_gain(LAST, 0, half)
+        centre_and_gain(LAST, half, DK)
+        scale_scalar(LAST, 0, half)
+        store(LAST, 0, half)
+        scale_scalar(LAST, half, DK)
+        store(LAST, half, DK)

@@ -22,19 +22,25 @@ TILES = T * M // P
 PASSES = D // 512
 PAIRS = DK // 2
 FREQS = PAIRS // 2
-W_LOADS = PAIRS // P
+BLOCKS = PAIRS // P
+HALF = DK // 2
 LAST = TILES - 1
-G_GAIN = 0
-G_NORM = 512
-LAG = 2
-
+SCALAR_STATS = (0, 5)
+ANGLE_GROUPS = ((0, 1), (1, 4), (4, 8))
+VECTOR_GAIN = (5, 6, 7)
+POS_GROUPS = ((0, 1), (1, 4), (4, 8))
+X_GROUPS = ((0, 1), (1, 2), (2, 4), (4, 6), (6, 8))
+ACC_BANKS = (2, 3)
+OUT_BANKS = (5, 6, 0, 1, 4, 7)
+IN_BANKS = (0, 1, 7, 4, 5, 6)
+W_GROUPS = ((0, 0, 1), (0, 1, 2), (0, 2, 4), (1, 0, 2), (1, 2, 4))
 
 def tile_attentionalsplatting_pa_kernel(tc, updated_track_tokens, tracks, W_k, k_gamma, out):
     nc = tc.nc
     x_rows = updated_track_tokens.flatten_outer_dims().rearrange("(p j) k -> p j k", j=TILES)
     pos_rows = tracks.flatten_outer_dims().rearrange("(p j) c -> p (j c)", j=TILES)
     out_rows = out.flatten_outer_dims().rearrange("(p j) n -> p j n", j=TILES)
-    w_rows = W_k.rearrange("(q p e) k -> q p e k", p=P, e=2)
+    w_rows = W_k.rearrange("(q p e) k -> e p q k", p=P, e=2)
 
     with ExitStack() as ctx:
         keep = ctx.enter_context(tc.tile_pool(name="keep", bufs=1))
@@ -42,237 +48,335 @@ def tile_attentionalsplatting_pa_kernel(tc, updated_track_tokens, tracks, W_k, k
         psum = ctx.enter_context(tc.psum_pool(name="psum", bufs=1))
         ctx.enter_context(tc.manual_schedule())
 
-        gamma_rows = keep.tile([P, DK], BF16, name="gamma_rows")
-        nc.vector.memset(gamma_rows[:], 0.0)
-        pos_bf = keep.tile([P, 2 * TILES], BF16, name="pos_bf")
-        nc.scalar.dma_start(out=pos_bf[:], in_=pos_rows)
-        nc.scalar.dma_start(out=gamma_rows[0:1, :], in_=k_gamma.rearrange("(o n) -> o n", o=1))
+        def bank(number, shape, dtype):
+            return psum.tile(shape, dtype, name="bank%d" % number)
 
-        w_raw = [keep.tile([P, 2, D], BF16, name="w_raw%d" % q) for q in range(W_LOADS)]
-        x_groups = [(0, 1), (1, 2), (2, 4), (4, 6), (6, 8)]
-        x_raw = [keep.tile([P, b - a, D], BF16, name="x_raw%d" % a) for a, b in x_groups]
-        x_src = {}
-        for (a, b), t in zip(x_groups, x_raw):
-            for j in range(a, b):
-                x_src[j] = t[:, j - a, :]
-        for q in range(W_LOADS - 1):
-            nc.sync.dma_start(out=w_raw[q][:], in_=w_rows[q])
-        nc.sync.dma_start(out=x_raw[0][:], in_=x_rows[:, 0:1, :])
-        nc.sync.dma_start(out=w_raw[W_LOADS - 1][:], in_=w_rows[W_LOADS - 1])
-        for (a, b), t in list(zip(x_groups, x_raw))[1:]:
+        pos = keep.tile([P, 2 * TILES], BF16, name="pos")
+        nc.scalar.dma_start(out=pos[:], in_=pos_rows)
+        raw = {}
+
+        def load_w(e, a, b):
+            t = keep.tile([P, b - a, D], BF16, name="w_raw%d%d" % (e, a))
+            nc.sync.dma_start(out=t[:], in_=w_rows[e, :, a:b, :])
+            for q in range(a, b):
+                raw[e, q] = t[:, q - a, :]
+
+        def load_x(a, b):
+            t = keep.tile([P, b - a, D], BF16, name="x_raw%d" % a)
             nc.sync.dma_start(out=t[:], in_=x_rows[:, a:b, :])
+            for j in range(a, b):
+                raw[j] = t[:, j - a, :]
+
+        for group in W_GROUPS[:3]:
+            load_w(*group)
+        load_x(*X_GROUPS[0])
+        for group in W_GROUPS[3:]:
+            load_w(*group)
+        for group in X_GROUPS[1:]:
+            load_x(*group)
+        gamma = keep.tile([P, DK], BF16, name="gamma")
+        nc.sync.dma_start(out=gamma[:], in_=k_gamma.partition_broadcast(P))
 
         ident = keep.tile([P, P], F32, name="ident")
         make_identity(nc, ident[:])
-        ones = keep.tile([P, P], BF16, name="ones")
-        nc.gpsimd.memset(ones[:], 1.0)
+        ident_bf = keep.tile([P, P], BF16, name="ident_bf")
+        nc.vector.tensor_copy(out=ident_bf[:], in_=ident[:])
+        index = keep.tile([P, 2], F32, name="index")
+        nc.gpsimd.iota(index[:], pattern=[[P, 2]], base=0, channel_multiplier=1, allow_small_or_imprecise_dtypes=True)
+        base = keep.tile([P, 2], F32, name="base")
+        nc.vector.memset(base[:], 100.0)
         minus_half = keep.tile([P, 1], F32, name="minus_half")
-        nc.gpsimd.memset(minus_half[:], -0.5)
+        nc.vector.memset(minus_half[:], -0.5)
+        stats = [keep.tile([P, 6 if j in SCALAR_STATS else 12], F32, name="stats%d" % j) for j in range(TILES)]
+        for j in SCALAR_STATS:
+            nc.vector.memset(stats[j][:, 0:6:3], float(HALF))
+        exponent = keep.tile([P, 2], F32, name="exponent")
+        nc.gpsimd.tensor_scalar(out=exponent[:], in0=index[:], scalar1=-1.0 / FREQS, scalar2=0.0, op0=ALU.mult, op1=ALU.add)
+        theta = keep.tile([P, 2], F32, name="theta")
+        nc.gpsimd.tensor_tensor(out=theta[:], in0=base[:], in1=exponent[:], op=ALU.pow)
+        turns = keep.tile([P, 2], F32, name="turns")
+        nc.gpsimd.tensor_scalar(out=turns[:], in0=theta[:], scalar1=1.0 / (2 * math.pi), scalar2=0.0, op0=ALU.mult, op1=ALU.add)
 
-        one = keep.tile([P, 1], F32, name="one")
-        nc.vector.memset(one[:], 1.0)
-        turns = keep.tile([P, FREQS], F32, name="turns")
-        for i in range(4):
-            nc.vector.tensor_scalar(out=turns[:, i : i + 1], in0=one[:], scalar1=100.0 ** (-i / FREQS) / (2 * math.pi), scalar2=None, op0=ALU.mult)
-        for width in (4, 16, 64):
-            for m in (1, 2, 3):
-                nc.vector.tensor_scalar(out=turns[:, m * width : (m + 1) * width], in0=turns[:, 0:width], scalar1=100.0 ** (-m * width / FREQS), scalar2=None, op0=ALU.mult)
-        pos = keep.tile([P, 2 * TILES], F32, name="pos")
-        nc.vector.tensor_copy(out=pos[:], in_=pos_bf[:])
+        pos_wide = keep.tile([P, 2 * TILES, P], BF16, name="pos_wide")
+        frac = keep.tile([P, 2 * TILES, 2, P], F32, name="frac")
+        codes, scales, turned, staged, spread, whole, fold = {}, {}, {}, {}, {}, {}, {}
+        trig, acc, prod_even, prod_odd, rotated, moments, rstd, shift, result = {}, {}, {}, {}, {}, {}, {}, {}, {}
 
+        def spread_pos(n):
+            a, b = POS_GROUPS[n]
+            spread[n] = bank(4 + n, [P, 2 * (b - a), P], BF16)
+            for c in range(2 * a, 2 * b):
+                nc.tensor.matmul(spread[n][:, c - 2 * a, :], lhsT=pos[:, c : c + 1].to_broadcast([P, P]), rhs=ident_bf[:], start=True, stop=True)
 
-        w_codes = keep.tile([P, 2, PASSES, PAIRS], U32, name="w_codes", align_bytes=64)
-        w_scales = keep.tile([P, 2, PASSES, PAIRS], U8, name="w_scales", align_bytes=64)
-        x_codes = [keep.tile([P, PASSES * P], U32, name="x_codes%d" % j, align_bytes=64) for j in range(TILES)]
-        x_scales = [keep.tile([P, PASSES * P], U8, name="x_scales%d" % j, align_bytes=64) for j in range(TILES)]
-        frac = [keep.tile([P, PAIRS], F32, name="frac%d" % j) for j in range(TILES)]
-        sums = [keep.tile([P, 4], F32, name="sums%d" % j) for j in range(TILES)]
-        neg_mean = [keep.tile([P, 1], F32, name="neg_mean%d" % j) for j in range(TILES)]
-        sum_sq = [keep.tile([P, 1], F32, name="sum_sq%d" % j) for j in range(TILES)]
-        rstd = [keep.tile([P, 1], F32, name="rstd%d" % j) for j in range(TILES)]
-        var, result = {}, {}
-        banks, staged, sin, cos, fold, acc, rot, cross = {}, {}, {}, {}, {}, {}, {}, {}
+        def copy_pos(n):
+            a, b = POS_GROUPS[n]
+            if n < 2:
+                nc.vector.tensor_copy(out=pos_wide[:, 2 * a : 2 * b, :], in_=spread[n][:])
+            else:
+                nc.scalar.copy(out=pos_wide[:, 2 * a : 2 * b, :], in_=spread[n][:])
 
-        def transpose(key, rows):
-            words = rows.bitcast(F32)
-            banks[key] = psum.tile([P, PASSES, 2, P], F32, name="turned", bufs=3)
-            for g in range(PASSES):
-                for u in range(2):
-                    nc.tensor.transpose(banks[key][:, g, u, :], words[:, 256 * g + u : 256 * (g + 1) : 2], ident[:])
+        def round_angles(n, engine=nc.vector):
+            a, b = ANGLE_GROUPS[n]
+            whole[n] = work.tile([P, 2, 2 * (b - a), P], I32, name="whole", bufs=2)
+            for g in range(2):
+                engine.tensor_scalar(out=whole[n][:, g, :, :], in0=pos_wide[:, 2 * a : 2 * b, :], scalar1=turns[:, g : g + 1], scalar2=0.0, op0=ALU.mult, op1=ALU.add)
 
-        def copy_out(key):
-            staged[key] = work.tile([P, D], BF16, name="staged", bufs=4, align_bytes=64)
-            nc.scalar.copy(out=staged[key][:].bitcast(F32).rearrange("p (g r u) -> p g r u", g=PASSES, u=2), in_=banks[key][:].rearrange("p g u r -> p g r u"))
+        def reduce_angles(n, g):
+            a, b = ANGLE_GROUPS[n]
+            nc.vector.scalar_tensor_tensor(out=frac[:, 2 * a : 2 * b, g, :], in0=pos_wide[:, 2 * a : 2 * b, :], scalar=turns[:, g : g + 1], in1=whole[n][:, g, :, :], op0=ALU.mult, op1=ALU.subtract)
 
-        def quantize_w(q, e):
-            for g in range(PASSES):
-                cols = slice(q * P, (q + 1) * P)
-                nc.vector.quantize_mx(out=w_codes[:, e, g, cols].bitcast(E5M2X4), scales=w_scales[:, e, g, cols], in_=staged[q, e][:, 512 * g : 512 * (g + 1)])
+        def angles(n):
+            round_angles(n)
+            reduce_angles(n, 0)
+            reduce_angles(n, 1)
 
-        def quantize_x(j):
-            nc.vector.quantize_mx(out=x_codes[j][:].bitcast(E5M2X4), scales=x_scales[j][:], in_=staged[j][:])
+        def tile_frac(j):
+            return frac[:, 2 * j : 2 * j + 2, :, :].rearrange("p h g t -> p (h g t)")
 
-        def reduce_angles(j):
-            whole = work.tile([P, PAIRS], I32, name="whole", bufs=2)
-            for h in range(2):
-                nc.vector.tensor_scalar(out=whole[:, h * FREQS : (h + 1) * FREQS], in0=turns[:], scalar1=pos[:, 2 * j + h : 2 * j + h + 1], scalar2=None, op0=ALU.mult)
-            for h in range(2):
-                cols = slice(h * FREQS, (h + 1) * FREQS)
-                nc.vector.scalar_tensor_tensor(out=frac[j][:, cols], in0=turns[:], scalar=pos[:, 2 * j + h : 2 * j + h + 1], in1=whole[:, cols], op0=ALU.mult, op1=ALU.subtract)
-
-        def sine(j):
-            sin[j] = work.tile([P, PAIRS], F32, name="sin", bufs=3)
-            nc.scalar.activation(out=sin[j][:], in_=frac[j][:], func=ACT.Sin, scale=2 * math.pi)
+        def sine(j, g=None):
+            if j not in trig:
+                trig[j] = work.tile([P, 2, PAIRS], F32, name="trig", bufs=5)
+            if g is None:
+                nc.scalar.activation(out=trig[j][:, 1, :], in_=tile_frac(j), func=ACT.Sin, scale=2 * math.pi)
+            else:
+                part = trig[j][:, 1, :].rearrange("p (h g t) -> p h g t", h=2, g=2)[:, :, g, :]
+                nc.scalar.activation(out=part, in_=frac[:, 2 * j : 2 * j + 2, g, :], func=ACT.Sin, scale=2 * math.pi)
 
         def absolute(j):
             fold[j] = work.tile([P, PAIRS], F32, name="fold", bufs=2)
-            nc.scalar.activation(out=fold[j][:], in_=frac[j][:], func=ACT.Abs)
+            nc.scalar.activation(out=fold[j][:], in_=tile_frac(j), func=ACT.Abs)
 
         def cosine(j):
-            cos[j] = work.tile([P, PAIRS], F32, name="cos", bufs=3)
-            nc.scalar.activation(out=cos[j][:], in_=fold[j][:], func=ACT.Sin, scale=-2 * math.pi, bias=math.pi / 2)
+            nc.scalar.activation(out=trig[j][:, 0, :], in_=fold[j][:], func=ACT.Sin, scale=-2 * math.pi, bias=math.pi / 2)
 
-        def project(j):
-            for e in range(2):
-                acc[j, e] = psum.tile([P, PAIRS], F32, name="acc%d" % e, bufs=2)
+        def tables(j):
+            absolute(j)
+            sine(j)
+            cosine(j)
+
+        def turn_in(key, number):
+            words = raw[key].bitcast(F32)
+            turned[key] = bank(number, [P, PASSES, 2, P], F32)
+            for g in range(PASSES):
+                for u in range(2):
+                    nc.tensor.transpose(turned[key][:, g, u, :], words[:, 256 * g + u : 256 * (g + 1) : 2], ident[:])
+
+        def copy_out(key):
+            staged[key] = work.tile([P, D], BF16, name="staged", bufs=8, align_bytes=64)
+            nc.scalar.copy(out=staged[key][:].bitcast(F32).rearrange("p (g r u) -> p g r u", g=PASSES, u=2), in_=turned[key][:].rearrange("p g u r -> p g r u"))
+
+        def quantize(key):
+            codes[key] = keep.tile([P, PASSES, P], U32, name="codes%s" % str(key).replace(" ", "").replace("(", "w").replace(")", "").replace(",", ""), align_bytes=64)
+            scales[key] = keep.tile([P, PASSES, P], U8, name="scales%s" % str(key).replace(" ", "").replace("(", "w").replace(")", "").replace(",", ""), align_bytes=64)
+            nc.vector.quantize_mx(out=codes[key][:].rearrange("p g c -> p (g c)").bitcast(E5M2X4), scales=scales[key][:].rearrange("p g c -> p (g c)"), in_=staged[key][:])
+
+        def project(j, e):
+            acc[j, e] = bank(ACC_BANKS[(2 * j + e) % len(ACC_BANKS)], [P, BLOCKS, P], F32)
+            for q in range(BLOCKS):
                 for g in range(PASSES):
-                    cols = slice(g * P, (g + 1) * P)
-                    nc.tensor.matmul_mx(out=acc[j, e][:], lhsT=x_codes[j][:, cols].bitcast(E5M2X4), lhsT_scale=x_scales[j][:, cols], rhs=w_codes[:, e, g, :].bitcast(E5M2X4), rhs_scale=w_scales[:, e, g, :], start=(g == 0), stop=(g == PASSES - 1))
+                    nc.tensor.matmul_mx(out=acc[j, e][:, q, :], lhsT=codes[e, q][:, g, :].bitcast(E5M2X4), lhsT_scale=scales[e, q][:, g, :], rhs=codes[j][:, g, :].bitcast(E5M2X4), rhs_scale=scales[j][:, g, :], start=(g == 0), stop=(g == PASSES - 1))
 
-        def multiply(j, e):
-            if e == 0:
-                rot[j] = work.tile([P, 2, PAIRS], F32, name="rot", bufs=4)
-                cross[j] = work.tile([P, 2, PAIRS], F32, name="cross")
-            terms = ((rot[j][:, e, :], e, 1.0, cos), (cross[j][:, e, :], 1 - e, 2.0 * e - 1.0, sin))
-            for n, (dst, bank, sign, table) in enumerate(terms):
-                nc.vector.scalar_tensor_tensor(out=dst, in0=acc[j, bank][:], scalar=sign, in1=table[j][:], op0=ALU.mult, op1=ALU.mult, accum_out=sums[j][:, 2 * e + n : 2 * e + n + 1])
+        def multiply_even(j, lo=0, hi=PAIRS):
+            if lo == 0:
+                prod_even[j] = work.tile([P, 2, PAIRS], F32, name="prod_even", bufs=2)
+            k_even = acc[j, 0][:].rearrange("p q t -> p (q t)")[:, lo:hi].unsqueeze(1).to_broadcast([P, 2, hi - lo])
+            nc.vector.tensor_tensor(out=prod_even[j][:, :, lo:hi], in0=k_even, in1=trig[j][:, :, lo:hi], op=ALU.mult)
 
-        def mean(j):
-            parts = work.tile([P, 4], F32, name="parts")
-            nc.scalar.activation(out=parts[:], in_=sums[j][:], func=ACT.Identity, scale=-1.0 / DK, accum_out=neg_mean[j][:])
+        def multiply_odd_sin(j, lo=0, hi=PAIRS):
+            if lo == 0:
+                prod_odd[j] = work.tile([P, 2, PAIRS], F32, name="prod_odd", bufs=2)
+            k_odd = acc[j, 1][:].rearrange("p q t -> p (q t)")[:, lo:hi]
+            nc.vector.scalar_tensor_tensor(out=prod_odd[j][:, 0, lo:hi], in0=k_odd, scalar=-1.0, in1=trig[j][:, 1, lo:hi], op0=ALU.mult, op1=ALU.mult)
 
-        def add(j, engine=nc.gpsimd, e=slice(0, 2)):
-            engine.tensor_tensor(out=rot[j][:, e, :], in0=rot[j][:, e, :], in1=cross[j][:, e, :], op=ALU.add)
+        def multiply_odd_cos(j, lo=0, hi=PAIRS):
+            k_odd = acc[j, 1][:].rearrange("p q t -> p (q t)")[:, lo:hi]
+            nc.vector.tensor_tensor(out=prod_odd[j][:, 1, lo:hi], in0=k_odd, in1=trig[j][:, 0, lo:hi], op=ALU.mult)
 
-        def square(j):
-            nc.scalar.activation(out=cross[j][:], in_=rot[j][:], func=ACT.Square, bias=neg_mean[j][:], accum_out=sum_sq[j][:])
+        def out_bank(j, h):
+            return OUT_BANKS[(2 * j + h) % len(OUT_BANKS)]
 
-        def variance(j):
-            var[j] = work.tile([P, 1], F32, name="var")
-            nc.scalar.activation(out=var[j][:], in_=sum_sq[j][:], func=ACT.Identity, scale=1.0 / DK, bias=EPS)
+        def turn_back(j, h):
+            rotated[j, h] = bank(out_bank(j, h), [P, 2, 2, P], F32)
+            for e in range(2):
+                for g in range(2):
+                    cols = slice((2 * h + g) * P, (2 * h + g + 1) * P)
+                    for n, prod in enumerate((prod_even[j], prod_odd[j])):
+                        nc.tensor.matmul(rotated[j, h][:, e, g, :], lhsT=prod[:, e, cols], rhs=ident[:], start=(n == 0), stop=(n == 1), is_transpose=True)
+
+        def flat(j, h):
+            return rotated[j, h][:].rearrange("p e g c -> p (e g c)")
+
+        def paired(j, h):
+            return rotated[j, h][:].rearrange("p e g c -> p (g c) e")
+
+        def stats_vector(j, h):
+            nc.vector.bn_stats(out=stats[j][:, 6 * h : 6 * h + 6], in_=flat(j, h))
+
+        def stats_scalar(j):
+            for h in range(2):
+                unused = work.tile([P, HALF], BF16, name="unused")
+                nc.scalar.activation(out=unused[:], in_=flat(j, h), func=ACT.Identity, scale=1.0 / HALF, accum_out=stats[j][:, 3 * h + 1 : 3 * h + 2])
+            for h in range(2):
+                unused = work.tile([P, HALF], BF16, name="unused")
+                nc.scalar.activation(out=unused[:], in_=flat(j, h), func=ACT.Square, scale=-1.0, bias=stats[j][:, 3 * h + 1 : 3 * h + 2], accum_out=stats[j][:, 3 * h + 2 : 3 * h + 3])
+
+        def aggregate(j):
+            moments[j] = keep.tile([P, 2], F32, name="moments%d" % j)
+            nc.vector.bn_aggr(out=moments[j][:], in_=stats[j][:])
 
         def inverse_std(j):
-            nc.gpsimd.tensor_tensor(out=rstd[j][:], in0=var[j][:], in1=minus_half[:], op=ALU.pow)
+            var = work.tile([P, 1], F32, name="var")
+            nc.gpsimd.tensor_scalar(out=var[:], in0=moments[j][:, 1:2], scalar1=1.0, scalar2=EPS, op0=ALU.mult, op1=ALU.add)
+            rstd[j] = keep.tile([P, 1], F32, name="rstd%d" % j)
+            nc.gpsimd.tensor_tensor(out=rstd[j][:], in0=var[:], in1=minus_half[:], op=ALU.pow)
 
-        def paired(j, lo, hi):
-            return rot[j][:, :, lo // 2 : hi // 2].rearrange("p e c -> p c e")
+        def mean_shift(j):
+            shift[j] = keep.tile([P, 1], F32, name="shift%d" % j)
+            nc.gpsimd.tensor_scalar(out=shift[j][:], in0=moments[j][:, 0:1], scalar1=rstd[j][:], scalar2=-1.0, op0=ALU.mult, op1=ALU.mult)
 
-        def centre_and_gain(j, lo=0, hi=DK):
-            if lo == 0:
-                result[j] = work.tile([P, DK], F32, name="result", bufs=4)
-            nc.vector.scalar_tensor_tensor(out=result[j][:, lo:hi], in0=paired(j, lo, hi), scalar=neg_mean[j][:], in1=gamma[:, lo:hi], op0=ALU.add, op1=ALU.mult)
+        def half_of(j, h):
+            if h == 0:
+                result[j] = work.tile([P, DK], F32, name="result", bufs=5)
+            return result[j][:, h * HALF : (h + 1) * HALF]
 
-        def scale_gpsimd(j, lo, hi):
-            if hi > lo:
-                nc.gpsimd.tensor_scalar(out=result[j][:, lo:hi], in0=result[j][:, lo:hi], scalar1=rstd[j][:], scalar2=0.0, op0=ALU.mult, op1=ALU.add)
+        def normalise(j, h):
+            nc.scalar.activation(out=half_of(j, h).rearrange("p (n e) -> p n e", e=2), in_=paired(j, h), func=ACT.Identity, scale=rstd[j][:], bias=shift[j][:])
+
+        def gain(j, engine, lo=0, hi=DK):
+            engine.tensor_tensor(out=result[j][:, lo:hi], in0=result[j][:, lo:hi], in1=gamma[:, lo:hi], op=ALU.mult)
+
+        def centre_and_gain(j, h):
+            nc.vector.scalar_tensor_tensor(out=half_of(j, h).rearrange("p (n e) -> p n e", e=2), in0=paired(j, h), scalar=moments[j][:, 0:1], in1=gamma[:, h * HALF : (h + 1) * HALF].rearrange("p (n e) -> p n e", e=2), op0=ALU.subtract, op1=ALU.mult)
+
+        def scale_vector(j, lo, hi):
+            nc.vector.tensor_scalar(out=result[j][:, lo:hi], in0=result[j][:, lo:hi], scalar1=rstd[j][:], scalar2=None, op0=ALU.mult)
 
         def scale_scalar(j, lo, hi):
-            if hi > lo:
-                nc.scalar.activation(out=result[j][:, lo:hi], in_=result[j][:, lo:hi], func=ACT.Identity, scale=rstd[j][:])
+            nc.scalar.activation(out=result[j][:, lo:hi], in_=result[j][:, lo:hi], func=ACT.Identity, scale=rstd[j][:])
 
         def store(j, lo=0, hi=DK):
             nc.sync.dma_start(out=out_rows[:, j, lo:hi], in_=result[j][:, lo:hi])
 
-        gamma = psum.tile([P, DK], BF16, name="gamma")
-        for half in range(2):
-            cols = slice(half * 512, (half + 1) * 512)
-            nc.tensor.matmul(gamma[:, cols], lhsT=ones[:], rhs=gamma_rows[:, cols], start=True, stop=True)
-        reduce_angles(0)
-        reduce_angles(1)
-        reduce_angles(2)
-        w_tiles = [(q, e) for q in range(W_LOADS) for e in range(2)]
-        trig_first = [sine, absolute, cosine]
-        for n, (q, e) in enumerate(w_tiles):
-            if n == len(w_tiles) - 2:
-                transpose(0, x_src[0])
-                copy_out(0)
-                quantize_x(0)
-            transpose((q, e), w_raw[q][:, e, :])
-            if n < 3:
-                trig_first[n](0)
-            copy_out((q, e))
-            quantize_w(q, e)
-            if n in (0, 1, 3):
-                reduce_angles({0: 3, 1: 4, 3: 5}[n])
-        transpose(1, x_src[1])
+        spread_pos(0)
+        spread_pos(1)
+        copy_pos(0)
+        round_angles(0)
+        reduce_angles(0, 0)
+        sine(0, 0)
+        copy_pos(1)
+        reduce_angles(0, 1)
+        first = [(0, q) for q in range(BLOCKS)] + [0] + [(1, q) for q in range(BLOCKS)]
+        in_bank = {key: IN_BANKS[n % len(IN_BANKS)] for n, key in enumerate(first + list(range(1, TILES)))}
+        for n, key in enumerate(first):
+            turn_in(key, in_bank[key])
+            if n == 1:
+                spread_pos(2)
+            copy_out(key)
+            if n == 0:
+                sine(0, 1)
+            if n == 2:
+                copy_pos(2)
+            if n == 0:
+                round_angles(1)
+            if n == 1:
+                reduce_angles(1, 0)
+            if n == 3:
+                reduce_angles(1, 1)
+            if n == 5:
+                round_angles(2)
+            if n == 7:
+                reduce_angles(2, 0)
+            quantize(key)
+            if n == BLOCKS * 2 - 1:
+                absolute(0)
+        cosine(0)
+        for j in range(1, 3 + 1):
+            turn_in(j, in_bank[j])
+        project(0, 0)
+        project(0, 1)
         copy_out(1)
-        project(0)
-        reduce_angles(6)
-        quantize_x(1)
-        absolute(1)
-        sine(1)
-        cosine(1)
-        transpose(2, x_src[2])
-        copy_out(2)
-        transpose(3, x_src[3])
-        copy_out(3)
-        reduce_angles(7)
-        project(1)
-        gains = {j: G_GAIN for j in range(TILES)}
+        tables(1)
+        for j in range(3 + 1, 7 + 1):
+            turn_in(j, in_bank[j])
+        for j in range(2, 7 + 1):
+            copy_out(j)
 
+        def finish(j):
+            aggregate(j)
+            inverse_std(j)
+            if j not in VECTOR_GAIN:
+                mean_shift(j)
+
+        def gain_rest(j):
+            if j >= 0 and j not in VECTOR_GAIN:
+                gain(j, nc.gpsimd, 0, DK)
+                if j + 1 not in VECTOR_GAIN:
+                    store(j)
+
+        def vector_gain(j):
+            for h in range(2):
+                centre_and_gain(j, h)
+            for h in range(2):
+                scale_scalar(j, h * HALF, (h + 1) * HALF)
+                store(j, h * HALF, (h + 1) * HALF)
 
         for s in range(TILES):
-            ahead = [j for j in (2 * s + 4, 2 * s + 5) if j < TILES]
-            for j in ahead:
-                transpose(j, x_src[j])
-            share = G_NORM if s + 2 < TILES else 0
-            if s >= 3:
-                scale_scalar(s - 3, share, DK)
-                scale_gpsimd(s - 3, 0, share)
-                store(s - 3)
-            multiply(s, 0)
-            if s >= 2:
-                inverse_std(s - 2)
-            if s == LAST:
-                add(s, nc.gpsimd, slice(0, 1))
-                centre_and_gain(s - 2)
-            multiply(s, 1)
-            for j in (2 * s + 2, 2 * s + 3):
-                if j < TILES:
-                    quantize_x(j)
-            if s + 2 < TILES:
-                project(s + 2)
-                absolute(s + 2)
-                sine(s + 2)
-                cosine(s + 2)
-            for j in ahead:
-                copy_out(j)
-            if s >= 1:
-                square(s - 1)
+
+            multiply_even(s)
+            if s >= 2 and s - 2 not in SCALAR_STATS:
+                finish(s - 2)
+                gain_rest(s - 3)
+
+            if s == 0:
+                quantize(1)
             if s < LAST:
-                mean(s)
-            if s >= 1:
-                variance(s - 1)
-            if 2 <= s < LAST:
-                centre_and_gain(s - 2)
+                project(s + 1, 0)
+            if 1 <= s < LAST:
+                tables(s + 1)
+            if s - 1 in SCALAR_STATS:
+                stats_scalar(s - 1)
+            multiply_odd_sin(s)
+
+            multiply_odd_cos(s)
+            if s - 2 in SCALAR_STATS:
+                finish(s - 2)
+                gain_rest(s - 3)
             if s < LAST:
-                add(s)
-        inverse_std(LAST - 1)
-        scale_scalar(LAST - 2, 0, DK)
-        store(LAST - 2)
-        mean(LAST)
-        add(LAST, nc.vector, slice(1, 2))
-        square(LAST)
-        centre_and_gain(LAST - 1)
-        scale_gpsimd(LAST - 1, 0, 512)
-        variance(LAST)
-        scale_scalar(LAST - 1, 512, DK)
-        store(LAST - 1)
-        inverse_std(LAST)
-        half = DK // 2
-        centre_and_gain(LAST, 0, half)
-        centre_and_gain(LAST, half, DK)
-        scale_scalar(LAST, 0, half)
-        store(LAST, 0, half)
-        scale_scalar(LAST, half, DK)
-        store(LAST, half, DK)
+                project(s + 1, 1)
+            if s == 0:
+                for j in range(7 + 1, TILES):
+                    turn_in(j, in_bank[j])
+                    copy_out(j)
+            turn_back(s, 0)
+            turn_back(s, 1)
+            if s == 0:
+                reduce_angles(2, 1)
+            for j in {0: (2,), 1: (3, 4, 5, 6, 7)}.get(s, ()):
+                quantize(j)
+
+            if s >= 1 and s - 1 not in SCALAR_STATS:
+                stats_vector(s - 1, 0)
+                if s - 2 in VECTOR_GAIN:
+                    vector_gain(s - 2)
+                    store(s - 3)
+                stats_vector(s - 1, 1)
+            if s >= 2 and s - 2 not in VECTOR_GAIN:
+                normalise(s - 2, 0)
+
+                normalise(s - 2, 1)
+        stats_vector(LAST, 0)
+        finish(LAST - 1)
+        stats_vector(LAST, 1)
+        centre_and_gain(LAST - 1, 0)
+        finish(LAST)
+        gain_rest(LAST - 2)
+        centre_and_gain(LAST - 1, 1)
+        for h in range(2):
+            scale_scalar(LAST - 1, h * HALF, (h + 1) * HALF)
+            store(LAST - 1, h * HALF, (h + 1) * HALF)
+        for h in range(2):
+            centre_and_gain(LAST, h)
+        scale_scalar(LAST, 0, HALF)
+        store(LAST, 0, HALF)
+        scale_vector(LAST, HALF, DK)
+        store(LAST, HALF, DK)

@@ -19,27 +19,33 @@ ACT = mybir.ActivationFunctionType
 
 P = 128
 TILES = T * M // P
-PASSES = D // 512
-PAIRS = DK // 2
-FREQS = PAIRS // 2
-BLOCKS = PAIRS // P
-HALF = DK // 2
 LAST = TILES - 1
-SCALAR_STATS = (0, 5)
+PASSES = D // 512
+PASS_WORDS = 256
+PAIRS = DK // 2
+BLOCKS = PAIRS // P
+FREQS = PAIRS // 2
+HALF = DK // 2
+
+W_LOADS = ((0, 0, 1), (0, 1, 2), (0, 2, 4), (1, 0, 2), (1, 2, 4))
+X_LOADS = ((0, 1), (1, 2), (2, 4), (4, 6), (6, 8))
 ANGLE_GROUPS = ((0, 1), (1, 4), (4, 8))
-VECTOR_GAIN = (5, 6, 7)
-POS_GROUPS = ((0, 1), (1, 4), (4, 8))
-X_GROUPS = ((0, 1), (1, 2), (2, 4), (4, 6), (6, 8))
+X_WIDE = (4, 5, 6, 7)
+
 ACC_BANKS = (2, 3)
-OUT_BANKS = (5, 6, 0, 1, 4, 7)
+POS_BANKS = (4, 5, 6)
 IN_BANKS = (0, 1, 7, 4, 5, 6)
-W_GROUPS = ((0, 0, 1), (0, 1, 2), (0, 2, 4), (1, 0, 2), (1, 2, 4))
+OUT_BANKS = (5, 6, 0, 1, 4, 7)
+
+SCALAR_STATS = (0, LAST - 2)
+FIRST_VECTOR_GAIN = LAST - 2
+
 
 def tile_attentionalsplatting_pa_kernel(tc, updated_track_tokens, tracks, W_k, k_gamma, out):
     nc = tc.nc
-    x_rows = updated_track_tokens.flatten_outer_dims().rearrange("(p j) k -> p j k", j=TILES)
-    pos_rows = tracks.flatten_outer_dims().rearrange("(p j) c -> p (j c)", j=TILES)
-    out_rows = out.flatten_outer_dims().rearrange("(p j) n -> p j n", j=TILES)
+    x_rows = updated_track_tokens.flatten_outer_dims().rearrange("(t j) k -> t j k", j=TILES)
+    pos_rows = tracks.flatten_outer_dims().rearrange("(t j) h -> t (j h)", j=TILES)
+    out_rows = out.flatten_outer_dims().rearrange("(t j) n -> t j n", j=TILES)
     w_rows = W_k.rearrange("(q p e) k -> e p q k", p=P, e=2)
 
     with ExitStack() as ctx:
@@ -51,29 +57,28 @@ def tile_attentionalsplatting_pa_kernel(tc, updated_track_tokens, tracks, W_k, k
         def bank(number, shape, dtype):
             return psum.tile(shape, dtype, name="bank%d" % number)
 
-        pos = keep.tile([P, 2 * TILES], BF16, name="pos")
-        nc.scalar.dma_start(out=pos[:], in_=pos_rows)
         raw = {}
 
-        def load_w(e, a, b):
-            t = keep.tile([P, b - a, D], BF16, name="w_raw%d%d" % (e, a))
-            nc.sync.dma_start(out=t[:], in_=w_rows[e, :, a:b, :])
-            for q in range(a, b):
-                raw[e, q] = t[:, q - a, :]
+        def load_w(e, first, end):
+            rows = keep.tile([P, end - first, D], BF16, name="w_raw%d%d" % (e, first))
+            nc.sync.dma_start(out=rows[:], in_=w_rows[e, :, first:end, :])
+            for q in range(first, end):
+                raw[e, q] = rows[:, q - first, :]
 
-        def load_x(a, b):
-            t = keep.tile([P, b - a, D], BF16, name="x_raw%d" % a)
-            nc.sync.dma_start(out=t[:], in_=x_rows[:, a:b, :])
-            for j in range(a, b):
-                raw[j] = t[:, j - a, :]
+        def load_x(first, end):
+            rows = keep.tile([P, end - first, D], BF16, name="x_raw%d" % first)
+            nc.sync.dma_start(out=rows[:], in_=x_rows[:, first:end, :])
+            for j in range(first, end):
+                raw[j] = rows[:, j - first, :]
 
-        for group in W_GROUPS[:3]:
-            load_w(*group)
-        load_x(*X_GROUPS[0])
-        for group in W_GROUPS[3:]:
-            load_w(*group)
-        for group in X_GROUPS[1:]:
-            load_x(*group)
+        pos = keep.tile([P, 2 * TILES], BF16, name="pos")
+        nc.sync.dma_start(out=pos[:], in_=pos_rows)
+        for load in W_LOADS:
+            if load[:2] == (1, 0):
+                load_x(*X_LOADS[0])
+            load_w(*load)
+        for load in X_LOADS[1:]:
+            load_x(*load)
         gamma = keep.tile([P, DK], BF16, name="gamma")
         nc.sync.dma_start(out=gamma[:], in_=k_gamma.partition_broadcast(P))
 
@@ -81,8 +86,8 @@ def tile_attentionalsplatting_pa_kernel(tc, updated_track_tokens, tracks, W_k, k
         make_identity(nc, ident[:])
         ident_bf = keep.tile([P, P], BF16, name="ident_bf")
         nc.vector.tensor_copy(out=ident_bf[:], in_=ident[:])
-        index = keep.tile([P, 2], F32, name="index")
-        nc.gpsimd.iota(index[:], pattern=[[P, 2]], base=0, channel_multiplier=1, allow_small_or_imprecise_dtypes=True)
+        freq_index = keep.tile([P, 2], F32, name="freq_index")
+        nc.gpsimd.iota(freq_index[:], pattern=[[P, 2]], base=0, channel_multiplier=1, allow_small_or_imprecise_dtypes=True)
         base = keep.tile([P, 2], F32, name="base")
         nc.vector.memset(base[:], 100.0)
         minus_half = keep.tile([P, 1], F32, name="minus_half")
@@ -91,56 +96,47 @@ def tile_attentionalsplatting_pa_kernel(tc, updated_track_tokens, tracks, W_k, k
         for j in SCALAR_STATS:
             nc.vector.memset(stats[j][:, 0:6:3], float(HALF))
         exponent = keep.tile([P, 2], F32, name="exponent")
-        nc.gpsimd.tensor_scalar(out=exponent[:], in0=index[:], scalar1=-1.0 / FREQS, scalar2=0.0, op0=ALU.mult, op1=ALU.add)
-        theta = keep.tile([P, 2], F32, name="theta")
-        nc.gpsimd.tensor_tensor(out=theta[:], in0=base[:], in1=exponent[:], op=ALU.pow)
+        nc.gpsimd.tensor_scalar(out=exponent[:], in0=freq_index[:], scalar1=-1.0 / FREQS, scalar2=-math.log(2 * math.pi) / math.log(100.0), op0=ALU.mult, op1=ALU.add)
         turns = keep.tile([P, 2], F32, name="turns")
-        nc.gpsimd.tensor_scalar(out=turns[:], in0=theta[:], scalar1=1.0 / (2 * math.pi), scalar2=0.0, op0=ALU.mult, op1=ALU.add)
+        nc.gpsimd.tensor_tensor(out=turns[:], in0=base[:], in1=exponent[:], op=ALU.pow)
 
         pos_wide = keep.tile([P, 2 * TILES, P], BF16, name="pos_wide")
         frac = keep.tile([P, 2 * TILES, 2, P], F32, name="frac")
-        codes, scales, turned, staged, spread, whole, fold = {}, {}, {}, {}, {}, {}, {}
-        trig, acc, prod_even, prod_odd, rotated, moments, rstd, shift, result = {}, {}, {}, {}, {}, {}, {}, {}, {}
+        staged_wide = keep.tile([P, len(X_WIDE), D], BF16, name="staged_wide", align_bytes=64)
+        spread, whole, fold, trig = {}, {}, {}, {}
+        turned, staged, codes, scales = {}, {}, {}, {}
+        acc, prod_even, prod_odd, rotated = {}, {}, {}, {}
+        moments, rstd, shift, result = {}, {}, {}, {}
 
-        def spread_pos(n):
-            a, b = POS_GROUPS[n]
-            spread[n] = bank(4 + n, [P, 2 * (b - a), P], BF16)
-            for c in range(2 * a, 2 * b):
-                nc.tensor.matmul(spread[n][:, c - 2 * a, :], lhsT=pos[:, c : c + 1].to_broadcast([P, P]), rhs=ident_bf[:], start=True, stop=True)
+        def spread_pos(group):
+            first, end = ANGLE_GROUPS[group]
+            spread[group] = bank(POS_BANKS[group], [P, 2 * (end - first), P], BF16)
+            for col in range(2 * first, 2 * end):
+                nc.tensor.matmul(spread[group][:, col - 2 * first, :], lhsT=pos[:, col : col + 1].to_broadcast([P, P]), rhs=ident_bf[:], start=True, stop=True)
 
-        def copy_pos(n):
-            a, b = POS_GROUPS[n]
-            if n < 2:
-                nc.vector.tensor_copy(out=pos_wide[:, 2 * a : 2 * b, :], in_=spread[n][:])
-            else:
-                nc.scalar.copy(out=pos_wide[:, 2 * a : 2 * b, :], in_=spread[n][:])
+        def group_pos(group):
+            first, end = ANGLE_GROUPS[group]
+            return pos_wide[:, 2 * first : 2 * end, :]
 
-        def round_angles(n, engine=nc.vector):
-            a, b = ANGLE_GROUPS[n]
-            whole[n] = work.tile([P, 2, 2 * (b - a), P], I32, name="whole", bufs=2)
+        def round_angles(group):
+            first, end = ANGLE_GROUPS[group]
+            whole[group] = work.tile([P, 2, 2 * (end - first), P], I32, name="whole", bufs=2)
             for g in range(2):
-                engine.tensor_scalar(out=whole[n][:, g, :, :], in0=pos_wide[:, 2 * a : 2 * b, :], scalar1=turns[:, g : g + 1], scalar2=0.0, op0=ALU.mult, op1=ALU.add)
+                nc.vector.tensor_scalar(out=whole[group][:, g, :, :], in0=group_pos(group), scalar1=turns[:, g : g + 1], scalar2=0.0, op0=ALU.mult, op1=ALU.add)
 
-        def reduce_angles(n, g):
-            a, b = ANGLE_GROUPS[n]
-            nc.vector.scalar_tensor_tensor(out=frac[:, 2 * a : 2 * b, g, :], in0=pos_wide[:, 2 * a : 2 * b, :], scalar=turns[:, g : g + 1], in1=whole[n][:, g, :, :], op0=ALU.mult, op1=ALU.subtract)
-
-        def angles(n):
-            round_angles(n)
-            reduce_angles(n, 0)
-            reduce_angles(n, 1)
+        def reduce_angles(group, g):
+            first, end = ANGLE_GROUPS[group]
+            nc.vector.scalar_tensor_tensor(out=frac[:, 2 * first : 2 * end, g, :], in0=group_pos(group), scalar=turns[:, g : g + 1], in1=whole[group][:, g, :, :], op0=ALU.mult, op1=ALU.subtract)
 
         def tile_frac(j):
             return frac[:, 2 * j : 2 * j + 2, :, :].rearrange("p h g t -> p (h g t)")
 
-        def sine(j, g=None):
-            if j not in trig:
-                trig[j] = work.tile([P, 2, PAIRS], F32, name="trig", bufs=5)
-            if g is None:
-                nc.scalar.activation(out=trig[j][:, 1, :], in_=tile_frac(j), func=ACT.Sin, scale=2 * math.pi)
-            else:
-                part = trig[j][:, 1, :].rearrange("p (h g t) -> p h g t", h=2, g=2)[:, :, g, :]
-                nc.scalar.activation(out=part, in_=frac[:, 2 * j : 2 * j + 2, g, :], func=ACT.Sin, scale=2 * math.pi)
+        def new_tables(j):
+            trig[j] = work.tile([P, 2, PAIRS], F32, name="trig", bufs=5)
+
+        def first_sine(g):
+            part = trig[0][:, 1, :].rearrange("p (h g t) -> p h g t", h=2, g=2)[:, :, g, :]
+            nc.scalar.activation(out=part, in_=frac[:, 0:2, g, :], func=ACT.Sin, scale=2 * math.pi)
 
         def absolute(j):
             fold[j] = work.tile([P, PAIRS], F32, name="fold", bufs=2)
@@ -151,232 +147,210 @@ def tile_attentionalsplatting_pa_kernel(tc, updated_track_tokens, tracks, W_k, k
 
         def tables(j):
             absolute(j)
-            sine(j)
+            new_tables(j)
+            nc.scalar.activation(out=trig[j][:, 1, :], in_=tile_frac(j), func=ACT.Sin, scale=2 * math.pi)
             cosine(j)
 
-        def turn_in(key, number):
+        def turn_in(key):
             words = raw[key].bitcast(F32)
-            turned[key] = bank(number, [P, PASSES, 2, P], F32)
-            for g in range(PASSES):
+            turned[key] = bank(in_bank[key], [P, PASSES, 2, P], F32)
+            for n in range(PASSES):
                 for u in range(2):
-                    nc.tensor.transpose(turned[key][:, g, u, :], words[:, 256 * g + u : 256 * (g + 1) : 2], ident[:])
+                    nc.tensor.transpose(turned[key][:, n, u, :], words[:, PASS_WORDS * n + u : PASS_WORDS * (n + 1) : 2], ident[:])
 
         def copy_out(key):
-            staged[key] = work.tile([P, D], BF16, name="staged", bufs=8, align_bytes=64)
-            nc.scalar.copy(out=staged[key][:].bitcast(F32).rearrange("p (g r u) -> p g r u", g=PASSES, u=2), in_=turned[key][:].rearrange("p g u r -> p g r u"))
+            if key in X_WIDE:
+                staged[key] = staged_wide[:, X_WIDE.index(key), :]
+            else:
+                staged[key] = work.tile([P, D], BF16, name="staged", bufs=8, align_bytes=64)[:]
+            nc.scalar.copy(out=staged[key].bitcast(F32).rearrange("p (n c u) -> p n c u", n=PASSES, u=2), in_=turned[key][:].rearrange("p n u c -> p n c u"))
 
-        def quantize(key):
-            codes[key] = keep.tile([P, PASSES, P], U32, name="codes%s" % str(key).replace(" ", "").replace("(", "w").replace(")", "").replace(",", ""), align_bytes=64)
-            scales[key] = keep.tile([P, PASSES, P], U8, name="scales%s" % str(key).replace(" ", "").replace("(", "w").replace(")", "").replace(",", ""), align_bytes=64)
-            nc.vector.quantize_mx(out=codes[key][:].rearrange("p g c -> p (g c)").bitcast(E5M2X4), scales=scales[key][:].rearrange("p g c -> p (g c)"), in_=staged[key][:])
+        def quantize(keys, source, label):
+            code_tile = keep.tile([P, len(keys), PASSES, P], U32, name="codes_" + label, align_bytes=64)
+            scale_tile = keep.tile([P, len(keys), PASSES, P], U8, name="scales_" + label, align_bytes=64)
+            nc.vector.quantize_mx(out=code_tile[:].rearrange("p i n c -> p (i n c)").bitcast(E5M2X4), scales=scale_tile[:].rearrange("p i n c -> p (i n c)"), in_=source)
+            for i, key in enumerate(keys):
+                codes[key], scales[key] = code_tile[:, i, :, :], scale_tile[:, i, :, :]
+
+        def quantize_one(key):
+            quantize([key], staged[key], "x%d" % key if isinstance(key, int) else "w%d%d" % key)
 
         def project(j, e):
-            acc[j, e] = bank(ACC_BANKS[(2 * j + e) % len(ACC_BANKS)], [P, BLOCKS, P], F32)
+            acc[j, e] = bank(ACC_BANKS[e], [P, BLOCKS, P], F32)
             for q in range(BLOCKS):
-                for g in range(PASSES):
-                    nc.tensor.matmul_mx(out=acc[j, e][:, q, :], lhsT=codes[e, q][:, g, :].bitcast(E5M2X4), lhsT_scale=scales[e, q][:, g, :], rhs=codes[j][:, g, :].bitcast(E5M2X4), rhs_scale=scales[j][:, g, :], start=(g == 0), stop=(g == PASSES - 1))
+                for n in range(PASSES):
+                    nc.tensor.matmul_mx(out=acc[j, e][:, q, :], lhsT=codes[e, q][:, n, :].bitcast(E5M2X4), lhsT_scale=scales[e, q][:, n, :], rhs=codes[j][:, n, :].bitcast(E5M2X4), rhs_scale=scales[j][:, n, :], start=(n == 0), stop=(n == PASSES - 1))
 
-        def multiply_even(j, lo=0, hi=PAIRS):
-            if lo == 0:
-                prod_even[j] = work.tile([P, 2, PAIRS], F32, name="prod_even", bufs=2)
-            k_even = acc[j, 0][:].rearrange("p q t -> p (q t)")[:, lo:hi].unsqueeze(1).to_broadcast([P, 2, hi - lo])
-            nc.vector.tensor_tensor(out=prod_even[j][:, :, lo:hi], in0=k_even, in1=trig[j][:, :, lo:hi], op=ALU.mult)
+        def multiply_even(j):
+            prod_even[j] = work.tile([P, 2, PAIRS], F32, name="prod_even", bufs=2)
+            a = acc[j, 0][:].rearrange("p q t -> p (q t)").unsqueeze(1).to_broadcast([P, 2, PAIRS])
+            nc.vector.tensor_tensor(out=prod_even[j][:], in0=a, in1=trig[j][:], op=ALU.mult)
 
-        def multiply_odd_sin(j, lo=0, hi=PAIRS):
-            if lo == 0:
-                prod_odd[j] = work.tile([P, 2, PAIRS], F32, name="prod_odd", bufs=2)
-            k_odd = acc[j, 1][:].rearrange("p q t -> p (q t)")[:, lo:hi]
-            nc.vector.scalar_tensor_tensor(out=prod_odd[j][:, 0, lo:hi], in0=k_odd, scalar=-1.0, in1=trig[j][:, 1, lo:hi], op0=ALU.mult, op1=ALU.mult)
+        def multiply_odd(j):
+            prod_odd[j] = work.tile([P, 2, PAIRS], F32, name="prod_odd", bufs=2)
+            b = acc[j, 1][:].rearrange("p q t -> p (q t)")
+            nc.vector.scalar_tensor_tensor(out=prod_odd[j][:, 0, :], in0=b, scalar=-1.0, in1=trig[j][:, 1, :], op0=ALU.mult, op1=ALU.mult)
+            nc.vector.tensor_tensor(out=prod_odd[j][:, 1, :], in0=b, in1=trig[j][:, 0, :], op=ALU.mult)
 
-        def multiply_odd_cos(j, lo=0, hi=PAIRS):
-            k_odd = acc[j, 1][:].rearrange("p q t -> p (q t)")[:, lo:hi]
-            nc.vector.tensor_tensor(out=prod_odd[j][:, 1, lo:hi], in0=k_odd, in1=trig[j][:, 0, lo:hi], op=ALU.mult)
-
-        def out_bank(j, h):
-            return OUT_BANKS[(2 * j + h) % len(OUT_BANKS)]
-
-        def turn_back(j, h):
-            rotated[j, h] = bank(out_bank(j, h), [P, 2, 2, P], F32)
-            for e in range(2):
-                for g in range(2):
-                    cols = slice((2 * h + g) * P, (2 * h + g + 1) * P)
-                    for n, prod in enumerate((prod_even[j], prod_odd[j])):
-                        nc.tensor.matmul(rotated[j, h][:, e, g, :], lhsT=prod[:, e, cols], rhs=ident[:], start=(n == 0), stop=(n == 1), is_transpose=True)
+        def turn_back(j):
+            for h in range(2):
+                rotated[j, h] = bank(OUT_BANKS[(2 * j + h) % len(OUT_BANKS)], [P, 2, 2, P], F32)
+                for e in range(2):
+                    for g in range(2):
+                        cols = slice((2 * h + g) * P, (2 * h + g + 1) * P)
+                        for term, prod in enumerate((prod_even[j], prod_odd[j])):
+                            nc.tensor.matmul(rotated[j, h][:, e, g, :], lhsT=prod[:, e, cols], rhs=ident[:], start=(term == 0), stop=(term == 1), is_transpose=True)
 
         def flat(j, h):
-            return rotated[j, h][:].rearrange("p e g c -> p (e g c)")
+            return rotated[j, h][:].rearrange("t e g p -> t (e g p)")
 
-        def paired(j, h):
-            return rotated[j, h][:].rearrange("p e g c -> p (g c) e")
+        def in_channel_order(j, h):
+            return rotated[j, h][:].rearrange("t e g p -> t (g p) e")
 
         def stats_vector(j, h):
             nc.vector.bn_stats(out=stats[j][:, 6 * h : 6 * h + 6], in_=flat(j, h))
 
         def stats_scalar(j):
             for h in range(2):
-                unused = work.tile([P, HALF], BF16, name="unused")
-                nc.scalar.activation(out=unused[:], in_=flat(j, h), func=ACT.Identity, scale=1.0 / HALF, accum_out=stats[j][:, 3 * h + 1 : 3 * h + 2])
+                unread = work.tile([P, HALF], BF16, name="unread")
+                nc.scalar.activation(out=unread[:], in_=flat(j, h), func=ACT.Identity, scale=1.0 / HALF, accum_out=stats[j][:, 3 * h + 1 : 3 * h + 2])
             for h in range(2):
-                unused = work.tile([P, HALF], BF16, name="unused")
-                nc.scalar.activation(out=unused[:], in_=flat(j, h), func=ACT.Square, scale=-1.0, bias=stats[j][:, 3 * h + 1 : 3 * h + 2], accum_out=stats[j][:, 3 * h + 2 : 3 * h + 3])
+                unread = work.tile([P, HALF], BF16, name="unread")
+                nc.scalar.activation(out=unread[:], in_=flat(j, h), func=ACT.Square, scale=-1.0, bias=stats[j][:, 3 * h + 1 : 3 * h + 2], accum_out=stats[j][:, 3 * h + 2 : 3 * h + 3])
 
-        def aggregate(j):
+        def finish_stats(j):
             moments[j] = keep.tile([P, 2], F32, name="moments%d" % j)
             nc.vector.bn_aggr(out=moments[j][:], in_=stats[j][:])
-
-        def inverse_std(j):
             var = work.tile([P, 1], F32, name="var")
             nc.gpsimd.tensor_scalar(out=var[:], in0=moments[j][:, 1:2], scalar1=1.0, scalar2=EPS, op0=ALU.mult, op1=ALU.add)
             rstd[j] = keep.tile([P, 1], F32, name="rstd%d" % j)
             nc.gpsimd.tensor_tensor(out=rstd[j][:], in0=var[:], in1=minus_half[:], op=ALU.pow)
+            if j < FIRST_VECTOR_GAIN:
+                shift[j] = keep.tile([P, 1], F32, name="shift%d" % j)
+                nc.gpsimd.tensor_scalar(out=shift[j][:], in0=moments[j][:, 0:1], scalar1=rstd[j][:], scalar2=-1.0, op0=ALU.mult, op1=ALU.mult)
 
-        def mean_shift(j):
-            shift[j] = keep.tile([P, 1], F32, name="shift%d" % j)
-            nc.gpsimd.tensor_scalar(out=shift[j][:], in0=moments[j][:, 0:1], scalar1=rstd[j][:], scalar2=-1.0, op0=ALU.mult, op1=ALU.mult)
+        def half(h):
+            return slice(h * HALF, (h + 1) * HALF)
 
-        def half_of(j, h):
-            if h == 0:
-                result[j] = work.tile([P, DK], F32, name="result", bufs=5)
-            return result[j][:, h * HALF : (h + 1) * HALF]
+        def pairs_of(tile, h):
+            return tile[:, half(h)].rearrange("t (n e) -> t n e", e=2)
 
-        def normalise(j, h):
-            nc.scalar.activation(out=half_of(j, h).rearrange("p (n e) -> p n e", e=2), in_=paired(j, h), func=ACT.Identity, scale=rstd[j][:], bias=shift[j][:])
+        def new_result(j):
+            result[j] = work.tile([P, DK], F32, name="result", bufs=5)
 
-        def gain(j, engine, lo=0, hi=DK):
-            engine.tensor_tensor(out=result[j][:, lo:hi], in0=result[j][:, lo:hi], in1=gamma[:, lo:hi], op=ALU.mult)
+        def normalise(j):
+            new_result(j)
+            for h in range(2):
+                nc.scalar.activation(out=pairs_of(result[j], h), in_=in_channel_order(j, h), func=ACT.Identity, scale=rstd[j][:], bias=shift[j][:])
+
+        def gain(j):
+            nc.gpsimd.tensor_tensor(out=result[j][:], in0=result[j][:], in1=gamma[:], op=ALU.mult)
 
         def centre_and_gain(j, h):
-            nc.vector.scalar_tensor_tensor(out=half_of(j, h).rearrange("p (n e) -> p n e", e=2), in0=paired(j, h), scalar=moments[j][:, 0:1], in1=gamma[:, h * HALF : (h + 1) * HALF].rearrange("p (n e) -> p n e", e=2), op0=ALU.subtract, op1=ALU.mult)
+            if h == 0:
+                new_result(j)
+            nc.vector.scalar_tensor_tensor(out=pairs_of(result[j], h), in0=in_channel_order(j, h), scalar=moments[j][:, 0:1], in1=pairs_of(gamma, h), op0=ALU.subtract, op1=ALU.mult)
 
-        def scale_vector(j, lo, hi):
-            nc.vector.tensor_scalar(out=result[j][:, lo:hi], in0=result[j][:, lo:hi], scalar1=rstd[j][:], scalar2=None, op0=ALU.mult)
+        def store(j, cols):
+            nc.sync.dma_start(out=out_rows[:, j, cols], in_=result[j][:, cols])
 
-        def scale_scalar(j, lo, hi):
-            nc.scalar.activation(out=result[j][:, lo:hi], in_=result[j][:, lo:hi], func=ACT.Identity, scale=rstd[j][:])
+        def scale_and_store(j, h):
+            nc.scalar.activation(out=result[j][:, half(h)], in_=result[j][:, half(h)], func=ACT.Identity, scale=rstd[j][:])
+            store(j, half(h))
 
-        def store(j, lo=0, hi=DK):
-            nc.sync.dma_start(out=out_rows[:, j, lo:hi], in_=result[j][:, lo:hi])
-
+        first_keys = [(0, q) for q in range(BLOCKS)] + [0] + [(1, q) for q in range(BLOCKS)]
+        in_bank = {key: IN_BANKS[n % len(IN_BANKS)] for n, key in enumerate(first_keys + list(range(1, TILES)))}
         spread_pos(0)
         spread_pos(1)
-        copy_pos(0)
+        nc.vector.tensor_copy(out=group_pos(0), in_=spread[0][:])
         round_angles(0)
         reduce_angles(0, 0)
-        sine(0, 0)
-        copy_pos(1)
+        new_tables(0)
+        first_sine(0)
+        nc.vector.tensor_copy(out=group_pos(1), in_=spread[1][:])
         reduce_angles(0, 1)
-        first = [(0, q) for q in range(BLOCKS)] + [0] + [(1, q) for q in range(BLOCKS)]
-        in_bank = {key: IN_BANKS[n % len(IN_BANKS)] for n, key in enumerate(first + list(range(1, TILES)))}
-        for n, key in enumerate(first):
-            turn_in(key, in_bank[key])
+        angle_pieces = {0: (round_angles, 1), 1: (reduce_angles, 1, 0), 3: (reduce_angles, 1, 1), 5: (round_angles, 2), 7: (reduce_angles, 2, 0)}
+        for n, key in enumerate(first_keys):
+            turn_in(key)
             if n == 1:
                 spread_pos(2)
             copy_out(key)
             if n == 0:
-                sine(0, 1)
+                first_sine(1)
             if n == 2:
-                copy_pos(2)
-            if n == 0:
-                round_angles(1)
-            if n == 1:
-                reduce_angles(1, 0)
-            if n == 3:
-                reduce_angles(1, 1)
-            if n == 5:
-                round_angles(2)
-            if n == 7:
-                reduce_angles(2, 0)
-            quantize(key)
-            if n == BLOCKS * 2 - 1:
+                nc.scalar.copy(out=group_pos(2), in_=spread[2][:])
+            if n in angle_pieces:
+                angle_pieces[n][0](*angle_pieces[n][1:])
+            quantize_one(key)
+            if n == len(first_keys) - 2:
                 absolute(0)
         cosine(0)
-        for j in range(1, 3 + 1):
-            turn_in(j, in_bank[j])
+        early = range(1, 4)
+        for j in early:
+            turn_in(j)
         project(0, 0)
         project(0, 1)
         copy_out(1)
         tables(1)
-        for j in range(3 + 1, 7 + 1):
-            turn_in(j, in_bank[j])
-        for j in range(2, 7 + 1):
+        for j in range(early.stop, TILES):
+            turn_in(j)
+        for j in range(2, TILES):
             copy_out(j)
 
-        def finish(j):
-            aggregate(j)
-            inverse_std(j)
-            if j not in VECTOR_GAIN:
-                mean_shift(j)
-
-        def gain_rest(j):
-            if j >= 0 and j not in VECTOR_GAIN:
-                gain(j, nc.gpsimd, 0, DK)
-                if j + 1 not in VECTOR_GAIN:
-                    store(j)
-
-        def vector_gain(j):
-            for h in range(2):
-                centre_and_gain(j, h)
-            for h in range(2):
-                scale_scalar(j, h * HALF, (h + 1) * HALF)
-                store(j, h * HALF, (h + 1) * HALF)
+        def finish_and_gain(s):
+            finish_stats(s - 2)
+            if s >= 3:
+                gain(s - 3)
+            if 3 <= s < LAST:
+                store(s - 3, slice(0, DK))
 
         for s in range(TILES):
-
             multiply_even(s)
             if s >= 2 and s - 2 not in SCALAR_STATS:
-                finish(s - 2)
-                gain_rest(s - 3)
-
+                finish_and_gain(s)
             if s == 0:
-                quantize(1)
+                quantize_one(1)
             if s < LAST:
                 project(s + 1, 0)
             if 1 <= s < LAST:
                 tables(s + 1)
             if s - 1 in SCALAR_STATS:
                 stats_scalar(s - 1)
-            multiply_odd_sin(s)
-
-            multiply_odd_cos(s)
+            multiply_odd(s)
             if s - 2 in SCALAR_STATS:
-                finish(s - 2)
-                gain_rest(s - 3)
+                finish_and_gain(s)
             if s < LAST:
                 project(s + 1, 1)
-            if s == 0:
-                for j in range(7 + 1, TILES):
-                    turn_in(j, in_bank[j])
-                    copy_out(j)
-            turn_back(s, 0)
-            turn_back(s, 1)
+            turn_back(s)
             if s == 0:
                 reduce_angles(2, 1)
-            for j in {0: (2,), 1: (3, 4, 5, 6, 7)}.get(s, ()):
-                quantize(j)
-
-            if s >= 1 and s - 1 not in SCALAR_STATS:
+            if s < 2:
+                quantize_one(s + 2)
+            if s == 1:
+                quantize(X_WIDE, staged_wide[:].rearrange("p j k -> p (j k)"), "wide")
+            if 1 <= s < LAST and s - 1 not in SCALAR_STATS:
                 stats_vector(s - 1, 0)
-                if s - 2 in VECTOR_GAIN:
-                    vector_gain(s - 2)
-                    store(s - 3)
                 stats_vector(s - 1, 1)
-            if s >= 2 and s - 2 not in VECTOR_GAIN:
-                normalise(s - 2, 0)
+            if 0 <= s - 2 < FIRST_VECTOR_GAIN:
+                normalise(s - 2)
 
-                normalise(s - 2, 1)
+        stats_vector(LAST - 1, 0)
+        centre_and_gain(LAST - 2, 0)
+        centre_and_gain(LAST - 2, 1)
+        scale_and_store(LAST - 2, 0)
+        scale_and_store(LAST - 2, 1)
+        store(LAST - 3, slice(0, DK))
+        stats_vector(LAST - 1, 1)
         stats_vector(LAST, 0)
-        finish(LAST - 1)
+        finish_stats(LAST - 1)
         stats_vector(LAST, 1)
         centre_and_gain(LAST - 1, 0)
-        finish(LAST)
-        gain_rest(LAST - 2)
+        finish_stats(LAST)
         centre_and_gain(LAST - 1, 1)
-        for h in range(2):
-            scale_scalar(LAST - 1, h * HALF, (h + 1) * HALF)
-            store(LAST - 1, h * HALF, (h + 1) * HALF)
-        for h in range(2):
-            centre_and_gain(LAST, h)
-        scale_scalar(LAST, 0, HALF)
-        store(LAST, 0, HALF)
-        scale_vector(LAST, HALF, DK)
-        store(LAST, HALF, DK)
+        scale_and_store(LAST - 1, 0)
+        scale_and_store(LAST - 1, 1)
+        centre_and_gain(LAST, 0)
+        centre_and_gain(LAST, 1)
+        scale_and_store(LAST, 0)
+        nc.vector.tensor_scalar(out=result[LAST][:, half(1)], in0=result[LAST][:, half(1)], scalar1=rstd[LAST][:], scalar2=None, op0=ALU.mult)
+        store(LAST, half(1))

import math
from contextlib import ExitStack

import concourse.mybir as mybir
from concourse.masks import make_identity

T, M, D, DK = 2, 512, 1024, 1024
EPS = 1e-6
FLOPS = 2 * T * M * D * DK

F32 = mybir.dt.float32
BF16 = mybir.dt.bfloat16
I32 = mybir.dt.int32
U32 = mybir.dt.uint32
U8 = mybir.dt.uint8
E5M2X4 = mybir.dt.float8_e5m2_x4
ALU = mybir.AluOpType
ACT = mybir.ActivationFunctionType

P = 128
TILES = T * M // P
LAST = TILES - 1
PASSES = D // 512
PASS_WORDS = 256
PAIRS = DK // 2
BLOCKS = PAIRS // P
FREQS = PAIRS // 2
HALF = DK // 2

W_LOADS = ((0, 0, 1), (0, 1, 2), (0, 2, 4), (1, 0, 2), (1, 2, 4))
X_LOADS = ((0, 1), (1, 2), (2, 4), (4, 6), (6, 8))
ANGLE_GROUPS = ((0, 1), (1, 4), (4, 8))
X_WIDE = (4, 5, 6, 7)

ACC_BANKS = (2, 3)
POS_BANKS = (4, 5, 6)
IN_BANKS = (0, 1, 7, 4, 5, 6)
OUT_BANKS = (5, 6, 0, 1, 4, 7)

SCALAR_STATS = (0, LAST - 2)
FIRST_VECTOR_GAIN = LAST - 2


def tile_attentionalsplatting_pa_kernel(tc, updated_track_tokens, tracks, W_k, k_gamma, out):
    nc = tc.nc
    x_rows = updated_track_tokens.flatten_outer_dims().rearrange("(t j) k -> t j k", j=TILES)
    pos_rows = tracks.flatten_outer_dims().rearrange("(t j) h -> t (j h)", j=TILES)
    out_rows = out.flatten_outer_dims().rearrange("(t j) n -> t j n", j=TILES)
    w_rows = W_k.rearrange("(q p e) k -> e p q k", p=P, e=2)

    with ExitStack() as ctx:
        keep = ctx.enter_context(tc.tile_pool(name="keep", bufs=1))
        work = ctx.enter_context(tc.tile_pool(name="work", bufs=3))
        psum = ctx.enter_context(tc.psum_pool(name="psum", bufs=1))
        ctx.enter_context(tc.manual_schedule())

        def bank(number, shape, dtype):
            return psum.tile(shape, dtype, name="bank%d" % number)

        raw = {}

        def load_w(e, first, end):
            rows = keep.tile([P, end - first, D], BF16, name="w_raw%d%d" % (e, first))
            nc.sync.dma_start(out=rows[:], in_=w_rows[e, :, first:end, :])
            for q in range(first, end):
                raw[e, q] = rows[:, q - first, :]

        def load_x(first, end):
            rows = keep.tile([P, end - first, D], BF16, name="x_raw%d" % first)
            nc.sync.dma_start(out=rows[:], in_=x_rows[:, first:end, :])
            for j in range(first, end):
                raw[j] = rows[:, j - first, :]

        pos = keep.tile([P, 2 * TILES], BF16, name="pos")
        nc.sync.dma_start(out=pos[:], in_=pos_rows)
        for load in W_LOADS:
            if load[:2] == (1, 0):
                load_x(*X_LOADS[0])
            load_w(*load)
        for load in X_LOADS[1:]:
            load_x(*load)
        gamma = keep.tile([P, DK], BF16, name="gamma")
        nc.sync.dma_start(out=gamma[:], in_=k_gamma.partition_broadcast(P))

        ident = keep.tile([P, P], F32, name="ident")
        make_identity(nc, ident[:])
        ident_bf = keep.tile([P, P], BF16, name="ident_bf")
        nc.vector.tensor_copy(out=ident_bf[:], in_=ident[:])
        freq_index = keep.tile([P, 2], F32, name="freq_index")
        nc.gpsimd.iota(freq_index[:], pattern=[[P, 2]], base=0, channel_multiplier=1, allow_small_or_imprecise_dtypes=True)
        base = keep.tile([P, 2], F32, name="base")
        nc.vector.memset(base[:], 100.0)
        minus_half = keep.tile([P, 1], F32, name="minus_half")
        nc.vector.memset(minus_half[:], -0.5)
        stats = [keep.tile([P, 6 if j in SCALAR_STATS else 12], F32, name="stats%d" % j) for j in range(TILES)]
        for j in SCALAR_STATS:
            nc.vector.memset(stats[j][:, 0:6:3], float(HALF))
        exponent = keep.tile([P, 2], F32, name="exponent")
        nc.gpsimd.tensor_scalar(out=exponent[:], in0=freq_index[:], scalar1=-1.0 / FREQS, scalar2=-math.log(2 * math.pi) / math.log(100.0), op0=ALU.mult, op1=ALU.add)
        turns = keep.tile([P, 2], F32, name="turns")
        nc.gpsimd.tensor_tensor(out=turns[:], in0=base[:], in1=exponent[:], op=ALU.pow)

        pos_wide = keep.tile([P, 2 * TILES, P], BF16, name="pos_wide")
        frac = keep.tile([P, 2 * TILES, 2, P], F32, name="frac")
        staged_wide = keep.tile([P, len(X_WIDE), D], BF16, name="staged_wide", align_bytes=64)
        spread, whole, fold, trig = {}, {}, {}, {}
        turned, staged, codes, scales = {}, {}, {}, {}
        acc, prod_even, prod_odd, rotated = {}, {}, {}, {}
        moments, rstd, shift, result = {}, {}, {}, {}

        def spread_pos(group):
            first, end = ANGLE_GROUPS[group]
            spread[group] = bank(POS_BANKS[group], [P, 2 * (end - first), P], BF16)
            for col in range(2 * first, 2 * end):
                nc.tensor.matmul(spread[group][:, col - 2 * first, :], lhsT=pos[:, col : col + 1].to_broadcast([P, P]), rhs=ident_bf[:], start=True, stop=True)

        def group_pos(group):
            first, end = ANGLE_GROUPS[group]
            return pos_wide[:, 2 * first : 2 * end, :]

        def round_angles(group):
            first, end = ANGLE_GROUPS[group]
            whole[group] = work.tile([P, 2, 2 * (end - first), P], I32, name="whole", bufs=2)
            for g in range(2):
                nc.vector.tensor_scalar(out=whole[group][:, g, :, :], in0=group_pos(group), scalar1=turns[:, g : g + 1], scalar2=0.0, op0=ALU.mult, op1=ALU.add)

        def reduce_angles(group, g):
            first, end = ANGLE_GROUPS[group]
            nc.vector.scalar_tensor_tensor(out=frac[:, 2 * first : 2 * end, g, :], in0=group_pos(group), scalar=turns[:, g : g + 1], in1=whole[group][:, g, :, :], op0=ALU.mult, op1=ALU.subtract)

        def tile_frac(j):
            return frac[:, 2 * j : 2 * j + 2, :, :].rearrange("p h g t -> p (h g t)")

        def new_tables(j):
            trig[j] = work.tile([P, 2, PAIRS], F32, name="trig", bufs=5)

        def first_sine(g):
            part = trig[0][:, 1, :].rearrange("p (h g t) -> p h g t", h=2, g=2)[:, :, g, :]
            nc.scalar.activation(out=part, in_=frac[:, 0:2, g, :], func=ACT.Sin, scale=2 * math.pi)

        def absolute(j):
            fold[j] = work.tile([P, PAIRS], F32, name="fold", bufs=2)
            nc.scalar.activation(out=fold[j][:], in_=tile_frac(j), func=ACT.Abs)

        def cosine(j):
            nc.scalar.activation(out=trig[j][:, 0, :], in_=fold[j][:], func=ACT.Sin, scale=-2 * math.pi, bias=math.pi / 2)

        def tables(j):
            absolute(j)
            new_tables(j)
            nc.scalar.activation(out=trig[j][:, 1, :], in_=tile_frac(j), func=ACT.Sin, scale=2 * math.pi)
            cosine(j)

        def turn_in(key):
            words = raw[key].bitcast(F32)
            turned[key] = bank(in_bank[key], [P, PASSES, 2, P], F32)
            for n in range(PASSES):
                for u in range(2):
                    nc.tensor.transpose(turned[key][:, n, u, :], words[:, PASS_WORDS * n + u : PASS_WORDS * (n + 1) : 2], ident[:])

        def copy_out(key):
            if key in X_WIDE:
                staged[key] = staged_wide[:, X_WIDE.index(key), :]
            else:
                staged[key] = work.tile([P, D], BF16, name="staged", bufs=8, align_bytes=64)[:]
            nc.scalar.copy(out=staged[key].bitcast(F32).rearrange("p (n c u) -> p n c u", n=PASSES, u=2), in_=turned[key][:].rearrange("p n u c -> p n c u"))

        def quantize(keys, source, label):
            code_tile = keep.tile([P, len(keys), PASSES, P], U32, name="codes_" + label, align_bytes=64)
            scale_tile = keep.tile([P, len(keys), PASSES, P], U8, name="scales_" + label, align_bytes=64)
            nc.vector.quantize_mx(out=code_tile[:].rearrange("p i n c -> p (i n c)").bitcast(E5M2X4), scales=scale_tile[:].rearrange("p i n c -> p (i n c)"), in_=source)
            for i, key in enumerate(keys):
                codes[key], scales[key] = code_tile[:, i, :, :], scale_tile[:, i, :, :]

        def quantize_one(key):
            quantize([key], staged[key], "x%d" % key if isinstance(key, int) else "w%d%d" % key)

        def project(j, e):
            acc[j, e] = bank(ACC_BANKS[e], [P, BLOCKS, P], F32)
            for q in range(BLOCKS):
                for n in range(PASSES):
                    nc.tensor.matmul_mx(out=acc[j, e][:, q, :], lhsT=codes[e, q][:, n, :].bitcast(E5M2X4), lhsT_scale=scales[e, q][:, n, :], rhs=codes[j][:, n, :].bitcast(E5M2X4), rhs_scale=scales[j][:, n, :], start=(n == 0), stop=(n == PASSES - 1))

        def multiply_even(j):
            prod_even[j] = work.tile([P, 2, PAIRS], F32, name="prod_even", bufs=2)
            a = acc[j, 0][:].rearrange("p q t -> p (q t)").unsqueeze(1).to_broadcast([P, 2, PAIRS])
            nc.vector.tensor_tensor(out=prod_even[j][:], in0=a, in1=trig[j][:], op=ALU.mult)

        def multiply_odd(j):
            prod_odd[j] = work.tile([P, 2, PAIRS], F32, name="prod_odd", bufs=2)
            b = acc[j, 1][:].rearrange("p q t -> p (q t)")
            nc.vector.scalar_tensor_tensor(out=prod_odd[j][:, 0, :], in0=b, scalar=-1.0, in1=trig[j][:, 1, :], op0=ALU.mult, op1=ALU.mult)
            nc.vector.tensor_tensor(out=prod_odd[j][:, 1, :], in0=b, in1=trig[j][:, 0, :], op=ALU.mult)

        def turn_back(j):
            for h in range(2):
                rotated[j, h] = bank(OUT_BANKS[(2 * j + h) % len(OUT_BANKS)], [P, 2, 2, P], F32)
                for e in range(2):
                    for g in range(2):
                        cols = slice((2 * h + g) * P, (2 * h + g + 1) * P)
                        for term, prod in enumerate((prod_even[j], prod_odd[j])):
                            nc.tensor.matmul(rotated[j, h][:, e, g, :], lhsT=prod[:, e, cols], rhs=ident[:], start=(term == 0), stop=(term == 1), is_transpose=True)

        def flat(j, h):
            return rotated[j, h][:].rearrange("t e g p -> t (e g p)")

        def in_channel_order(j, h):
            return rotated[j, h][:].rearrange("t e g p -> t (g p) e")

        def stats_vector(j, h):
            nc.vector.bn_stats(out=stats[j][:, 6 * h : 6 * h + 6], in_=flat(j, h))

        def stats_scalar(j):
            for h in range(2):
                unread = work.tile([P, HALF], BF16, name="unread")
                nc.scalar.activation(out=unread[:], in_=flat(j, h), func=ACT.Identity, scale=1.0 / HALF, accum_out=stats[j][:, 3 * h + 1 : 3 * h + 2])
            for h in range(2):
                unread = work.tile([P, HALF], BF16, name="unread")
                nc.scalar.activation(out=unread[:], in_=flat(j, h), func=ACT.Square, scale=-1.0, bias=stats[j][:, 3 * h + 1 : 3 * h + 2], accum_out=stats[j][:, 3 * h + 2 : 3 * h + 3])

        def finish_stats(j):
            moments[j] = keep.tile([P, 2], F32, name="moments%d" % j)
            nc.vector.bn_aggr(out=moments[j][:], in_=stats[j][:])
            var = work.tile([P, 1], F32, name="var")
            nc.gpsimd.tensor_scalar(out=var[:], in0=moments[j][:, 1:2], scalar1=1.0, scalar2=EPS, op0=ALU.mult, op1=ALU.add)
            rstd[j] = keep.tile([P, 1], F32, name="rstd%d" % j)
            nc.gpsimd.tensor_tensor(out=rstd[j][:], in0=var[:], in1=minus_half[:], op=ALU.pow)
            if j < FIRST_VECTOR_GAIN:
                shift[j] = keep.tile([P, 1], F32, name="shift%d" % j)
                nc.gpsimd.tensor_scalar(out=shift[j][:], in0=moments[j][:, 0:1], scalar1=rstd[j][:], scalar2=-1.0, op0=ALU.mult, op1=ALU.mult)

        def half(h):
            return slice(h * HALF, (h + 1) * HALF)

        def pairs_of(tile, h):
            return tile[:, half(h)].rearrange("t (n e) -> t n e", e=2)

        def new_result(j):
            result[j] = work.tile([P, DK], F32, name="result", bufs=5)

        def normalise(j):
            new_result(j)
            for h in range(2):
                nc.scalar.activation(out=pairs_of(result[j], h), in_=in_channel_order(j, h), func=ACT.Identity, scale=rstd[j][:], bias=shift[j][:])

        def gain(j):
            nc.gpsimd.tensor_tensor(out=result[j][:], in0=result[j][:], in1=gamma[:], op=ALU.mult)

        def centre_and_gain(j, h):
            if h == 0:
                new_result(j)
            nc.vector.scalar_tensor_tensor(out=pairs_of(result[j], h), in0=in_channel_order(j, h), scalar=moments[j][:, 0:1], in1=pairs_of(gamma, h), op0=ALU.subtract, op1=ALU.mult)

        def store(j, cols):
            nc.sync.dma_start(out=out_rows[:, j, cols], in_=result[j][:, cols])

        def scale_and_store(j, h):
            nc.scalar.activation(out=result[j][:, half(h)], in_=result[j][:, half(h)], func=ACT.Identity, scale=rstd[j][:])
            store(j, half(h))

        first_keys = [(0, q) for q in range(BLOCKS)] + [0] + [(1, q) for q in range(BLOCKS)]
        in_bank = {key: IN_BANKS[n % len(IN_BANKS)] for n, key in enumerate(first_keys + list(range(1, TILES)))}
        spread_pos(0)
        spread_pos(1)
        nc.vector.tensor_copy(out=group_pos(0), in_=spread[0][:])
        round_angles(0)
        reduce_angles(0, 0)
        new_tables(0)
        first_sine(0)
        nc.vector.tensor_copy(out=group_pos(1), in_=spread[1][:])
        reduce_angles(0, 1)
        angle_pieces = {0: (round_angles, 1), 1: (reduce_angles, 1, 0), 3: (reduce_angles, 1, 1), 5: (round_angles, 2), 7: (reduce_angles, 2, 0)}
        for n, key in enumerate(first_keys):
            turn_in(key)
            if n == 1:
                spread_pos(2)
            copy_out(key)
            if n == 0:
                first_sine(1)
            if n == 2:
                nc.scalar.copy(out=group_pos(2), in_=spread[2][:])
            if n in angle_pieces:
                angle_pieces[n][0](*angle_pieces[n][1:])
            quantize_one(key)
            if n == len(first_keys) - 2:
                absolute(0)
        cosine(0)
        early = range(1, 4)
        for j in early:
            turn_in(j)
        project(0, 0)
        project(0, 1)
        copy_out(1)
        tables(1)
        for j in range(early.stop, TILES):
            turn_in(j)
        for j in range(2, TILES):
            copy_out(j)

        def finish_and_gain(s):
            finish_stats(s - 2)
            if s >= 3:
                gain(s - 3)
            if 3 <= s < LAST:
                store(s - 3, slice(0, DK))

        for s in range(TILES):
            multiply_even(s)
            if s >= 2 and s - 2 not in SCALAR_STATS:
                finish_and_gain(s)
            if s == 0:
                quantize_one(1)
            if s < LAST:
                project(s + 1, 0)
            if 1 <= s < LAST:
                tables(s + 1)
            if s - 1 in SCALAR_STATS:
                stats_scalar(s - 1)
            multiply_odd(s)
            if s - 2 in SCALAR_STATS:
                finish_and_gain(s)
            if s < LAST:
                project(s + 1, 1)
            turn_back(s)
            if s == 0:
                reduce_angles(2, 1)
            if s < 2:
                quantize_one(s + 2)
            if s == 1:
                quantize(X_WIDE, staged_wide[:].rearrange("p j k -> p (j k)"), "wide")
            if 1 <= s < LAST and s - 1 not in SCALAR_STATS:
                stats_vector(s - 1, 0)
                stats_vector(s - 1, 1)
            if 0 <= s - 2 < FIRST_VECTOR_GAIN:
                normalise(s - 2)

        stats_vector(LAST - 1, 0)
        centre_and_gain(LAST - 2, 0)
        centre_and_gain(LAST - 2, 1)
        scale_and_store(LAST - 2, 0)
        scale_and_store(LAST - 2, 1)
        store(LAST - 3, slice(0, DK))
        stats_vector(LAST - 1, 1)
        stats_vector(LAST, 0)
        finish_stats(LAST - 1)
        stats_vector(LAST, 1)
        centre_and_gain(LAST - 1, 0)
        finish_stats(LAST)
        centre_and_gain(LAST - 1, 1)
        scale_and_store(LAST - 1, 0)
        scale_and_store(LAST - 1, 1)
        centre_and_gain(LAST, 0)
        centre_and_gain(LAST, 1)
        scale_and_store(LAST, 0)
        nc.vector.tensor_scalar(out=result[LAST][:, half(1)], in0=result[LAST][:, half(1)], scalar1=rstd[LAST][:], scalar2=None, op0=ALU.mult)
        store(LAST, half(1))
